import numpy as np
import ml_dtypes


def mxq(x, axis, fmt="e4m3"):
    dtype, down = {"e4m3": (ml_dtypes.float8_e4m3fn, 7), "e5m2": (ml_dtypes.float8_e5m2, 14)}[fmt]
    v = np.moveaxis(np.asarray(x, np.float32).astype(ml_dtypes.bfloat16).astype(np.float64), axis, -1)
    blocks = v.reshape(v.shape[:-1] + (-1, 32))
    amax = np.abs(blocks).max(-1, keepdims=True)
    byte = np.maximum(np.where(amax > 0, np.frexp(amax)[1] - 1 + 127, 0) - down, 1)
    scale = np.exp2(byte - 127.0)
    codes = (blocks / scale).astype(np.float32).astype(dtype).astype(np.float64)
    return np.moveaxis((codes * scale).reshape(v.shape), -1, axis)


WIDE = False


def mx_kscale(k):
    if not WIDE:
        return np.ones(k)
    levels = np.array([10, -10, 5, -5, 0])
    a = np.random.permutation(np.resize(levels, k // 512 * 4)).reshape(k // 512, 4)
    idx = np.arange(k)
    return np.exp2(a[idx // 512, idx % 128 // 32])


BF16 = ml_dtypes.bfloat16


def bf(x):
    return np.asarray(x, np.float32).astype(BF16)


def f64(x):
    return np.asarray(x).astype(np.float64)


E2M1 = np.array([0.0, 0.5, 1.0, 1.5, 2.0, 3.0, 4.0, 6.0, -0.0, -0.5, -1.0, -1.5, -2.0, -3.0, -4.0, -6.0])


def pack_weight(w, fmt):
    k, n = w.shape
    w = f64(bf(w)).reshape(k // 32, 32, n)
    amax = np.abs(w).max(1)
    if fmt == "e4m3":
        byte = np.frexp(amax)[1] - 1 + 127 - 7
    else:
        mant, ex = np.frexp(amax / 6.0)
        byte = np.where(mant > 0.5, ex, ex - 1) + 127
    byte = np.clip(np.where(amax > 0, byte, 1), 1, 254)
    scaled = (w * np.exp2(127.0 - byte)[:, None, :]).reshape(k, n).astype(np.float32)
    by_word = np.ascontiguousarray(scaled.reshape(k // 512, 128, 4, n).transpose(0, 1, 3, 2))
    if fmt == "e4m3":
        words = by_word.astype(ml_dtypes.float8_e4m3fn).view(np.uint8)
    else:
        c = by_word.astype(ml_dtypes.float4_e2m1fn).view(np.uint8) & 0xF
        words = c[..., 0::2] | (c[..., 1::2] << 4)
    return np.ascontiguousarray(words), np.ascontiguousarray(byte.astype(np.uint8).reshape(k // 512, 16, n))


def unpack_weight(words, scales, fmt):
    g, p, n, _ = words.shape
    if fmt == "e4m3":
        vals = np.ascontiguousarray(words).view(ml_dtypes.float8_e4m3fn).astype(np.float64)
    else:
        nib = np.empty((g, p, n, 4), np.uint8)
        nib[..., 0::2] = words & 0xF
        nib[..., 1::2] = words >> 4
        vals = E2M1[nib]
    vals = vals * np.repeat(np.exp2(scales.astype(np.float64) - 127.0), 8, axis=1)[..., None]
    return vals.transpose(0, 1, 3, 2).reshape(g * 512, n)

def pack4(w):
    words, scales = pack_weight(w, "e2m1")
    return words.reshape(words.shape[0], 128, -1), scales


def unpack4(words, scales):
    return unpack_weight(words.reshape(words.shape[0], 128, -1, 2), scales, "e2m1")


B, S, D, NH, NKV, HD = 4, 4096, 512, 2, 1, 32
EPS = 1e-6
QS = NH * HD
KS = NKV * HD
E = QS + KS + KS
HP = HD // 2


def rmsnorm(v, w):
    ms = np.mean(np.square(v), axis=-1, keepdims=True)
    return v * (1.0 / np.sqrt(ms + EPS)) * w


def apply_rotary_emb(v, fc):
    vs = v.reshape(*v.shape[:-1], HP, 2)
    f = fc[None, :, None, :, :]
    vr, vi = vs[..., 0], vs[..., 1]
    fr, fi = f[..., 0], f[..., 1]
    return np.stack([vr * fr - vi * fi, vi * fr + vr * fi], axis=-1).reshape(v.shape)


def setup_inputs():
    s = mx_kscale(D)
    x = bf(np.random.standard_normal((B, S, D)) * s)
    freqs_cis = bf(np.random.standard_normal((S, HP, 2)))
    wqkv = np.random.standard_normal((E, D)) / np.sqrt(D) / s[None, :]
    words, scales = pack4(np.ascontiguousarray(wqkv.T))
    q_norm_w = bf(1.0 + 0.1 * np.random.standard_normal(HD))
    k_norm_w = bf(1.0 + 0.1 * np.random.standard_normal(HD))
    return {"x": x,
            "freqs_cis": freqs_cis,
            "wqkv_words": words,
            "wqkv_scales": scales,
            "q_norm_w": q_norm_w,
            "k_norm_w": k_norm_w}


def reference(x, freqs_cis, wqkv_words, wqkv_scales, q_norm_w, k_norm_w):
    fc = f64(freqs_cis)
    qkv = mxq(f64(x), 2, "e4m3") @ unpack4(wqkv_words, wqkv_scales)
    q = qkv[..., :QS].reshape(B, S, NH, HD)
    k = qkv[..., QS:QS + KS].reshape(B, S, NKV, HD)
    v = qkv[..., QS + KS:].reshape(B, S, NKV, HD)
    q = rmsnorm(q, f64(q_norm_w))
    k = rmsnorm(k, f64(k_norm_w))
    q_rot = apply_rotary_emb(q, fc)
    k_rot = apply_rotary_emb(k, fc)
    return q_rot, k_rot, v

@@ -1,0 +1,284 @@
+from contextlib import ExitStack
+import math
+
+import concourse.mybir as mybir
+from concourse.masks import make_identity
+
+F32 = mybir.dt.float32
+BF16 = mybir.dt.bfloat16
+I32 = mybir.dt.int32
+U32 = mybir.dt.uint32
+U8 = mybir.dt.uint8
+FP8X4 = mybir.dt.float8_e4m3fn_x4
+FP4X4 = mybir.dt.float4_e2m1fn_x4
+ACT = mybir.ActivationFunctionType
+ALU = mybir.AluOpType
+AXIS = mybir.AxisListType
+
+P = 128
+BATCH, SEQ, DIM = 4, 4096, 512
+HEAD = 32
+PAIRS = HEAD // 2
+NORMED = 3
+ROT = NORMED * HEAD
+ROT_PAIRS = NORMED * PAIRS
+QKV = ROT + HEAD
+EPS = 1e-6
+
+POS = SEQ // P
+GROUP = 4
+GROUPS = BATCH * POS // GROUP
+CHUNK = 2 * GROUP
+WORDS = DIM // 2
+LOOKAHEAD = 6
+
+FLOPS = 2 * BATCH * SEQ * DIM * QKV
+
+
+def tile_attention_pa_t_kernel(
+    tc, x, freqs_cis, wqkv_words, wqkv_scales, q_norm_w, k_norm_w, out_0, out_1, out_2
+):
+    nc = tc.nc
+    with ExitStack() as ctx:
+        const = ctx.enter_context(tc.tile_pool(name="const", bufs=1))
+        x_pool = ctx.enter_context(tc.tile_pool(name="x_pool", bufs=LOOKAHEAD + 2))
+        work = ctx.enter_context(tc.tile_pool(name="work", bufs=3))
+        psum_xt = ctx.enter_context(tc.psum_pool(name="psum_xt", bufs=4))
+        psum_qkv = ctx.enter_context(tc.psum_pool(name="psum_qkv", bufs=4))
+        ctx.enter_context(tc.manual_schedule())
+
+        x_rows = x.rearrange("b (p t) d -> b p t d", t=POS)
+        q_rows = out_0.rearrange("b (p t) h c -> b p t (h c)", t=POS)
+        k_rows = out_1.rearrange("b (p t) h c -> b p t (h c)", t=POS)
+        v_rows = out_2.rearrange("b (p t) h c -> b p t (h c)", t=POS)
+
+        live = {}
+
+        def load_x(g):
+            b, first = divmod(g * GROUP, POS)
+            x_tile = x_pool.tile([P, GROUP, DIM], BF16, name="x_tile")
+            live["x", g] = x_tile
+            nc.sync.dma_start(out=x_tile[:], in_=x_rows[b, :, first : first + GROUP, :])
+
+        gain_raw = const.tile([P, NORMED, HEAD], BF16)
+        nc.sync.dma_start(out=gain_raw[:, 0, :], in_=q_norm_w.partition_broadcast(P))
+        nc.sync.dma_start(out=gain_raw[:, 2, :], in_=k_norm_w.partition_broadcast(P))
+        fc = const.tile([P, POS, PAIRS, 2], BF16)
+        nc.sync.dma_start(out=fc[:], in_=freqs_cis.rearrange("(p t) j e -> p t j e", t=POS))
+        load_x(0)
+        w_words = const.tile([P, 2 * QKV], U8, align_bytes=64)
+        nc.sync.dma_start(out=w_words[:].bitcast(I32), in_=wqkv_words[0].bitcast(I32))
+        w_scales = const.tile([P, QKV], U8, align_bytes=64)
+        nc.vector.memset(w_scales[:].bitcast(I32), 0)
+        for quad in range(4):
+            nc.sync.dma_start(
+                out=w_scales[32 * quad : 32 * quad + 4, :].bitcast(I32),
+                in_=wqkv_scales[0, 4 * quad : 4 * quad + 4, :].bitcast(I32),
+            )
+        for g in range(1, LOOKAHEAD):
+            load_x(g)
+
+        ident = const.tile([P, P], F32)
+        make_identity(nc, ident[:])
+        eps = const.tile([P, 1], F32)
+        nc.vector.memset(eps[:], EPS)
+
+        nc.vector.tensor_copy(out=gain_raw[:, 1, :], in_=gain_raw[:, 0, :])
+        gain_pairs = gain_raw[:].rearrange("p h (j e) -> p h j e", e=2)
+        gain_minus = const.tile([P, NORMED, PAIRS], BF16)
+        nc.vector.tensor_scalar_mul(out=gain_minus[:], in0=gain_pairs[:, :, :, 1], scalar1=-1.0)
+        table_a = const.tile([P, 2, POS, ROT_PAIRS], F32)
+        table_b = const.tile([P, 2, POS, ROT_PAIRS], F32)
+
+        def build_tables(engine, first, count):
+            shape = [P, count, NORMED, PAIRS]
+            fr = fc[:, first : first + count, :, 0].unsqueeze(2).to_broadcast(shape)
+            fi = fc[:, first : first + count, :, 1].unsqueeze(2).to_broadcast(shape)
+            g_even = gain_pairs[:, :, :, 0].unsqueeze(1).to_broadcast(shape)
+            g_odd = gain_pairs[:, :, :, 1].unsqueeze(1).to_broadcast(shape)
+            g_minus = gain_minus[:].unsqueeze(1).to_broadcast(shape)
+            for table, which, f, g in (
+                (table_a, 0, fr, g_even),
+                (table_a, 1, fi, g_even),
+                (table_b, 0, fi, g_minus),
+                (table_b, 1, fr, g_odd),
+            ):
+                engine.tensor_tensor(
+                    out=table[:, which, first : first + count, :].rearrange(
+                        "p t (h j) -> p t h j", h=NORMED
+                    ),
+                    in0=f,
+                    in1=g,
+                    op=ALU.mult,
+                )
+
+        build_tables(nc.vector, 0, POS // 2)
+        build_tables(nc.gpsimd, POS // 2, POS // 2)
+
+        def transpose_x(g):
+            words = live["x", g][:].bitcast(F32)
+            for half in range(2):
+                xt = psum_xt.tile([P, 2, 2, P], F32, name="xt")
+                live["xt", g, half] = xt
+                for i in range(2):
+                    for u in range(2):
+                        nc.tensor.transpose(
+                            xt[:, i, u, :], words[:, 2 * half + i, u:WORDS:2], ident[:]
+                        )
+
+        def regroup_x(g):
+            grouped = work.tile([P, GROUP * P * 4], BF16, name="grouped", align_bytes=64)
+            live["grouped", g] = grouped
+            as_words = grouped[:].bitcast(F32).rearrange("p (i r u) -> p i r u", i=GROUP, u=2)
+            for half in range(2):
+                nc.scalar.copy(
+                    out=as_words[:, 2 * half : 2 * half + 2, :, :],
+                    in_=live["xt", g, half][:].rearrange("p i u r -> p i r u"),
+                )
+
+        def quantise_x(g):
+            codes = work.tile([P, GROUP * P], U32, name="codes", align_bytes=64)
+            planes = work.tile([P, GROUP * P], U8, name="planes", align_bytes=64)
+            live["codes", g] = (codes, planes)
+            nc.vector.quantize_mx(
+                out=codes[:].bitcast(FP8X4), scales=planes[:], in_=live["grouped", g][:]
+            )
+
+        def project(g):
+            codes, planes = live["codes", g]
+            qkv = psum_qkv.tile([P, GROUP, QKV], F32, name="qkv")
+            live["qkv", g] = qkv
+            for i in range(GROUP):
+                tokens = slice(i * P, (i + 1) * P)
+                nc.tensor.matmul_mx(
+                    out=qkv[:, i, :],
+                    lhsT=codes[:, tokens].bitcast(FP8X4),
+                    lhsT_scale=planes[:, tokens],
+                    rhs=w_words[:].bitcast(FP4X4),
+                    rhs_scale=w_scales[:],
+                    start=True,
+                    stop=True,
+                )
+
+        def chunk_tile(name, g, shape):
+            c, first = divmod(g * GROUP, CHUNK)
+            if (name, c) not in live:
+                live[name, c] = work.tile(shape, F32, name=name)
+            return live[name, c], slice(first, first + GROUP)
+
+        def hbm_rows(c):
+            b, first = divmod(c * CHUNK, POS)
+            return b, slice(first, first + CHUNK)
+
+        def squares_and_v(g):
+            qkv = live["qkv", g]
+            squares, rows = chunk_tile("squares", g, [P, CHUNK, ROT])
+            nc.scalar.activation(
+                out=squares[:, rows, :],
+                in_=qkv[:, :, 0:ROT],
+                func=ACT.Square,
+                scale=1.0 / math.sqrt(HEAD),
+            )
+            v_stage, rows = chunk_tile("v_stage", g, [P, CHUNK, HEAD])
+            nc.scalar.copy(out=v_stage[:, rows, :], in_=qkv[:, :, ROT:QKV])
+
+        def products(g):
+            first = g * GROUP % POS
+            pairs = live["qkv", g][:, :, 0:ROT].rearrange("p i (n e) -> p i n e", e=2)
+            prod, rows = chunk_tile("prod", g, [P, 4, CHUNK, ROT_PAIRS])
+            shape = [P, 2, GROUP, ROT_PAIRS]
+            nc.vector.tensor_tensor(
+                out=prod[:, 0:4:2, rows, :],
+                in0=pairs[:, :, :, 0].unsqueeze(1).to_broadcast(shape),
+                in1=table_a[:, :, first : first + GROUP, :],
+                op=ALU.mult,
+            )
+            nc.vector.tensor_tensor(
+                out=prod[:, 1:4:2, rows, :],
+                in0=pairs[:, :, :, 1].unsqueeze(1).to_broadcast(shape),
+                in1=table_b[:, :, first : first + GROUP, :],
+                op=ALU.mult,
+            )
+
+        def store_v(c):
+            b, rows = hbm_rows(c)
+            nc.sync.dma_start(out=v_rows[b, :, rows, :], in_=live["v_stage", c][:])
+
+        def mean_squares(c):
+            mean_sq = work.tile([P, CHUNK * NORMED], F32, name="mean_sq")
+            live["mean_sq", c] = mean_sq
+            nc.vector.tensor_reduce(
+                out=mean_sq[:],
+                in_=live["squares", c][:].rearrange("p i (h c) -> p (i h) c", c=HEAD),
+                axis=AXIS.X,
+                op=ALU.add,
+            )
+
+        def root(c):
+            rms = work.tile([P, CHUNK * NORMED], F32, name="rms")
+            live["rms", c] = rms
+            nc.scalar.activation(
+                out=rms[:], in_=live["mean_sq", c][:], func=ACT.Sqrt, bias=eps[:, 0:1], scale=1.0
+            )
+
+        def inverse(c):
+            inv_rms = work.tile([P, CHUNK, NORMED], F32, name="inv_rms")
+            live["inv_rms", c] = inv_rms
+            nc.vector.reciprocal(
+                out=inv_rms[:].rearrange("p i h -> p (i h)"), in_=live["rms", c][:]
+            )
+
+        def rotate(c):
+            prod = live["prod", c]
+            rotated = work.tile([P, CHUNK, ROT], F32, name="rotated")
+            live["rotated", c] = rotated
+            nc.gpsimd.tensor_tensor(
+                out=rotated[:].rearrange("p i (n e) -> p (i n) e", e=2),
+                in0=prod[:, 0:4:3].rearrange("p e i n -> p (i n) e"),
+                in1=prod[:, 1:3].rearrange("p e i n -> p (i n) e"),
+                op=ALU.add,
+            )
+
+        def norm_and_store(c):
+            rotated = live["rotated", c]
+            inv_rms = live["inv_rms", c]
+            b, rows = hbm_rows(c)
+            q_stage = work.tile([P, CHUNK, 2 * HEAD], F32, name="q_stage")
+            nc.gpsimd.tensor_tensor(
+                out=q_stage[:].rearrange("p i (h c) -> p i h c", c=HEAD),
+                in0=rotated[:, :, 0 : 2 * HEAD].rearrange("p i (h c) -> p i h c", c=HEAD),
+                in1=inv_rms[:, :, 0:2].unsqueeze(3).to_broadcast([P, CHUNK, 2, HEAD]),
+                op=ALU.mult,
+            )
+            k_stage = work.tile([P, CHUNK, HEAD], F32, name="k_stage")
+            nc.vector.tensor_tensor(
+                out=k_stage[:],
+                in0=rotated[:, :, 2 * HEAD : ROT],
+                in1=inv_rms[:, :, 2:3].to_broadcast([P, CHUNK, HEAD]),
+                op=ALU.mult,
+            )
+            nc.sync.dma_start(out=k_rows[b, :, rows, :], in_=k_stage[:])
+            nc.sync.dma_start(out=q_rows[b, :, rows, :], in_=q_stage[:])
+
+        def run(stage_fn, g):
+            if 0 <= g < GROUPS:
+                stage_fn(g)
+
+        def run_chunk(stage_fn, g):
+            if 0 <= g < GROUPS and g % 2 == 1:
+                stage_fn(g // 2)
+
+        for step in range(GROUPS + 4):
+            run(load_x, step + LOOKAHEAD)
+            run(transpose_x, step)
+            run(quantise_x, step - 1)
+            run(project, step - 1)
+            run(squares_and_v, step - 2)
+            run_chunk(store_v, step - 2)
+            run_chunk(mean_squares, step - 2)
+            run_chunk(root, step - 3)
+            run(regroup_x, step)
+            run_chunk(inverse, step - 3)
+            run(products, step - 2)
+            run_chunk(rotate, step - 3)
+            run_chunk(norm_and_store, step - 4)

@@ -31,6 +31,7 @@ GROUPS = BATCH * POS // GROUP
 CHUNK = 2 * GROUP
 WORDS = DIM // 2
 LOOKAHEAD = 6
+TABLE_PARTS = 4
 
 FLOPS = 2 * BATCH * SEQ * DIM * QKV
 
@@ -90,7 +91,9 @@ def tile_attention_pa_t_kernel(
         table_a = const.tile([P, 2, POS, ROT_PAIRS], F32)
         table_b = const.tile([P, 2, POS, ROT_PAIRS], F32)
 
-        def build_tables(engine, first, count):
+        def build_tables(part):
+            count = POS // TABLE_PARTS
+            first = part * count
             shape = [P, count, NORMED, PAIRS]
             fr = fc[:, first : first + count, :, 0].unsqueeze(2).to_broadcast(shape)
             fi = fc[:, first : first + count, :, 1].unsqueeze(2).to_broadcast(shape)
@@ -103,7 +106,7 @@ def tile_attention_pa_t_kernel(
                 (table_b, 0, fi, g_minus),
                 (table_b, 1, fr, g_odd),
             ):
-                engine.tensor_tensor(
+                nc.vector.tensor_tensor(
                     out=table[:, which, first : first + count, :].rearrange(
                         "p t (h j) -> p t h j", h=NORMED
                     ),
@@ -112,8 +115,8 @@ def tile_attention_pa_t_kernel(
                     op=ALU.mult,
                 )
 
-        build_tables(nc.vector, 0, POS // 2)
-        build_tables(nc.gpsimd, POS // 2, POS // 2)
+        build_tables(0)
+        build_tables(1)
 
         def transpose_x(g):
             words = live["x", g][:].bitcast(F32)
@@ -166,119 +169,100 @@ def tile_attention_pa_t_kernel(
                 live[name, c] = work.tile(shape, F32, name=name)
             return live[name, c], slice(first, first + GROUP)
 
-        def hbm_rows(c):
-            b, first = divmod(c * CHUNK, POS)
-            return b, slice(first, first + CHUNK)
-
-        def squares_and_v(g):
+        def statistics(g):
             qkv = live["qkv", g]
-            squares, rows = chunk_tile("squares", g, [P, CHUNK, ROT])
+            squares = work.tile([P, GROUP, NORMED, HEAD], F32, name="squares")
+            mean_sq = work.tile([P, GROUP, NORMED], F32, name="mean_sq")
+            for i in range(GROUP):
+                for h in range(NORMED):
+                    nc.scalar.activation(
+                        out=squares[:, i, h, :],
+                        in_=qkv[:, i, h * HEAD : (h + 1) * HEAD],
+                        func=ACT.Square,
+                        scale=1.0 / math.sqrt(HEAD),
+                        accum_out=mean_sq[:, i, h : h + 1],
+                    )
+            inv_rms = work.tile([P, GROUP, NORMED], F32, name="inv_rms")
+            live["inv_rms", g] = inv_rms
             nc.scalar.activation(
-                out=squares[:, rows, :],
-                in_=qkv[:, :, 0:ROT],
-                func=ACT.Square,
-                scale=1.0 / math.sqrt(HEAD),
+                out=inv_rms[:], in_=mean_sq[:], func=ACT.Abs_reciprocal_sqrt, bias=eps[:, 0:1], scale=1.0
             )
-            v_stage, rows = chunk_tile("v_stage", g, [P, CHUNK, HEAD])
-            nc.scalar.copy(out=v_stage[:, rows, :], in_=qkv[:, :, ROT:QKV])
+
+        def store_if_full(hbm, staged, g):
+            if g % 2 == 1:
+                b, first = divmod((g - 1) * GROUP, POS)
+                nc.sync.dma_start(out=hbm[b, :, first : first + CHUNK, :], in_=staged[:])
 
         def products(g):
             first = g * GROUP % POS
             pairs = live["qkv", g][:, :, 0:ROT].rearrange("p i (n e) -> p i n e", e=2)
-            prod, rows = chunk_tile("prod", g, [P, 4, CHUNK, ROT_PAIRS])
+            prod = work.tile([P, 4, GROUP, ROT_PAIRS], F32, name="prod")
+            live["prod", g] = prod
             shape = [P, 2, GROUP, ROT_PAIRS]
             nc.vector.tensor_tensor(
-                out=prod[:, 0:4:2, rows, :],
+                out=prod[:, 0:4:2],
                 in0=pairs[:, :, :, 0].unsqueeze(1).to_broadcast(shape),
                 in1=table_a[:, :, first : first + GROUP, :],
                 op=ALU.mult,
             )
             nc.vector.tensor_tensor(
-                out=prod[:, 1:4:2, rows, :],
+                out=prod[:, 1:4:2],
                 in0=pairs[:, :, :, 1].unsqueeze(1).to_broadcast(shape),
                 in1=table_b[:, :, first : first + GROUP, :],
                 op=ALU.mult,
             )
 
-        def store_v(c):
-            b, rows = hbm_rows(c)
-            nc.sync.dma_start(out=v_rows[b, :, rows, :], in_=live["v_stage", c][:])
+        def copy_v(g):
+            v_stage, rows = chunk_tile("v_stage", g, [P, CHUNK, HEAD])
+            nc.vector.tensor_copy(out=v_stage[:, rows, :], in_=live["qkv", g][:, :, ROT:QKV])
+            store_if_full(v_rows, v_stage, g)
 
-        def mean_squares(c):
-            mean_sq = work.tile([P, CHUNK * NORMED], F32, name="mean_sq")
-            live["mean_sq", c] = mean_sq
-            nc.vector.tensor_reduce(
-                out=mean_sq[:],
-                in_=live["squares", c][:].rearrange("p i (h c) -> p (i h) c", c=HEAD),
-                axis=AXIS.X,
-                op=ALU.add,
-            )
-
-        def root(c):
-            rms = work.tile([P, CHUNK * NORMED], F32, name="rms")
-            live["rms", c] = rms
-            nc.scalar.activation(
-                out=rms[:], in_=live["mean_sq", c][:], func=ACT.Sqrt, bias=eps[:, 0:1], scale=1.0
-            )
-
-        def inverse(c):
-            inv_rms = work.tile([P, CHUNK, NORMED], F32, name="inv_rms")
-            live["inv_rms", c] = inv_rms
-            nc.vector.reciprocal(
-                out=inv_rms[:].rearrange("p i h -> p (i h)"), in_=live["rms", c][:]
-            )
-
-        def rotate(c):
-            prod = live["prod", c]
-            rotated = work.tile([P, CHUNK, ROT], F32, name="rotated")
-            live["rotated", c] = rotated
-            nc.gpsimd.tensor_tensor(
+        def rotate(g):
+            prod = live["prod", g]
+            rotated = work.tile([P, GROUP, ROT], F32, name="rotated")
+            live["rotated", g] = rotated
+            nc.vector.tensor_tensor(
                 out=rotated[:].rearrange("p i (n e) -> p (i n) e", e=2),
                 in0=prod[:, 0:4:3].rearrange("p e i n -> p (i n) e"),
                 in1=prod[:, 1:3].rearrange("p e i n -> p (i n) e"),
                 op=ALU.add,
             )
 
-        def norm_and_store(c):
-            rotated = live["rotated", c]
-            inv_rms = live["inv_rms", c]
-            b, rows = hbm_rows(c)
-            q_stage = work.tile([P, CHUNK, 2 * HEAD], F32, name="q_stage")
+        def norm_q(g):
+            q_stage, rows = chunk_tile("q_stage", g, [P, CHUNK, 2 * HEAD])
             nc.gpsimd.tensor_tensor(
-                out=q_stage[:].rearrange("p i (h c) -> p i h c", c=HEAD),
-                in0=rotated[:, :, 0 : 2 * HEAD].rearrange("p i (h c) -> p i h c", c=HEAD),
-                in1=inv_rms[:, :, 0:2].unsqueeze(3).to_broadcast([P, CHUNK, 2, HEAD]),
+                out=q_stage[:, rows, :].rearrange("p i (h c) -> p i h c", c=HEAD),
+                in0=live["rotated", g][:, :, 0 : 2 * HEAD].rearrange("p i (h c) -> p i h c", c=HEAD),
+                in1=live["inv_rms", g][:, :, 0:2].unsqueeze(3).to_broadcast([P, GROUP, 2, HEAD]),
                 op=ALU.mult,
             )
-            k_stage = work.tile([P, CHUNK, HEAD], F32, name="k_stage")
+            store_if_full(q_rows, q_stage, g)
+
+        def norm_k(g):
+            k_stage, rows = chunk_tile("k_stage", g, [P, CHUNK, HEAD])
             nc.vector.tensor_tensor(
-                out=k_stage[:],
-                in0=rotated[:, :, 2 * HEAD : ROT],
-                in1=inv_rms[:, :, 2:3].to_broadcast([P, CHUNK, HEAD]),
+                out=k_stage[:, rows, :],
+                in0=live["rotated", g][:, :, 2 * HEAD : ROT],
+                in1=live["inv_rms", g][:, :, 2:3].to_broadcast([P, GROUP, HEAD]),
                 op=ALU.mult,
             )
-            nc.sync.dma_start(out=k_rows[b, :, rows, :], in_=k_stage[:])
-            nc.sync.dma_start(out=q_rows[b, :, rows, :], in_=q_stage[:])
+            store_if_full(k_rows, k_stage, g)
 
         def run(stage_fn, g):
             if 0 <= g < GROUPS:
                 stage_fn(g)
-
-        def run_chunk(stage_fn, g):
-            if 0 <= g < GROUPS and g % 2 == 1:
-                stage_fn(g // 2)
 
         for step in range(GROUPS + 4):
             run(load_x, step + LOOKAHEAD)
             run(transpose_x, step)
             run(quantise_x, step - 1)
             run(project, step - 1)
-            run(squares_and_v, step - 2)
-            run_chunk(store_v, step - 2)
-            run_chunk(mean_squares, step - 2)
-            run_chunk(root, step - 3)
+            if 2 <= step + 1 < TABLE_PARTS:
+                build_tables(step + 1)
+            run(norm_k, step - 4)
+            run(rotate, step - 3)
+            run(norm_q, step - 3)
+            run(statistics, step - 2)
             run(regroup_x, step)
-            run_chunk(inverse, step - 3)
             run(products, step - 2)
-            run_chunk(rotate, step - 3)
-            run_chunk(norm_and_store, step - 4)
+            run(copy_v, step - 2)

@@ -252,17 +252,22 @@ def tile_attention_pa_t_kernel(
             if 0 <= g < GROUPS:
                 stage_fn(g)
 
-        for step in range(GROUPS + 4):
+        def run_pair(stage_fn, g):
+            if 0 <= g < GROUPS and g % 2 == 1:
+                stage_fn(g - 1)
+                stage_fn(g)
+
+        for step in range(GROUPS + 5):
             run(load_x, step + LOOKAHEAD)
             run(transpose_x, step)
             run(quantise_x, step - 1)
-            run(project, step - 1)
+            run_pair(project, step - 1)
             if 2 <= step + 1 < TABLE_PARTS:
                 build_tables(step + 1)
-            run(norm_k, step - 4)
-            run(rotate, step - 3)
-            run(norm_q, step - 3)
-            run(statistics, step - 2)
+            run(norm_k, step - 5)
+            run(rotate, step - 4)
+            run(norm_q, step - 4)
+            run(statistics, step - 3)
             run(regroup_x, step)
-            run(products, step - 2)
-            run(copy_v, step - 2)
+            run(products, step - 3)
+            run(copy_v, step - 3)

@@ -91,7 +91,7 @@ def tile_attention_pa_t_kernel(
         table_a = const.tile([P, 2, POS, ROT_PAIRS], F32)
         table_b = const.tile([P, 2, POS, ROT_PAIRS], F32)
 
-        def build_tables(part):
+        def build_tables(part, engine):
             count = POS // TABLE_PARTS
             first = part * count
             shape = [P, count, NORMED, PAIRS]
@@ -106,7 +106,7 @@ def tile_attention_pa_t_kernel(
                 (table_b, 0, fi, g_minus),
                 (table_b, 1, fr, g_odd),
             ):
-                nc.vector.tensor_tensor(
+                engine.tensor_tensor(
                     out=table[:, which, first : first + count, :].rearrange(
                         "p t (h j) -> p t h j", h=NORMED
                     ),
@@ -115,8 +115,10 @@ def tile_attention_pa_t_kernel(
                     op=ALU.mult,
                 )
 
-        build_tables(0)
-        build_tables(1)
+        build_tables(0, nc.vector)
+        build_tables(1, nc.vector)
+        build_tables(2, nc.gpsimd)
+        build_tables(3, nc.gpsimd)
 
         def transpose_x(g):
             words = live["x", g][:].bitcast(F32)
@@ -169,23 +171,44 @@ def tile_attention_pa_t_kernel(
                 live[name, c] = work.tile(shape, F32, name=name)
             return live[name, c], slice(first, first + GROUP)
 
-        def statistics(g):
+        def square(g):
             qkv = live["qkv", g]
             squares = work.tile([P, GROUP, NORMED, HEAD], F32, name="squares")
             mean_sq = work.tile([P, GROUP, NORMED], F32, name="mean_sq")
+            live["squares", g] = squares
+            live["mean_sq", g] = mean_sq
+            nc.scalar.activation(
+                out=squares[:, :, 0:2, :],
+                in_=qkv[:, :, 0 : 2 * HEAD].rearrange("p i (h c) -> p i h c", c=HEAD),
+                func=ACT.Square,
+                scale=1.0 / math.sqrt(HEAD),
+            )
             for i in range(GROUP):
-                for h in range(NORMED):
-                    nc.scalar.activation(
-                        out=squares[:, i, h, :],
-                        in_=qkv[:, i, h * HEAD : (h + 1) * HEAD],
-                        func=ACT.Square,
-                        scale=1.0 / math.sqrt(HEAD),
-                        accum_out=mean_sq[:, i, h : h + 1],
-                    )
+                nc.scalar.activation(
+                    out=squares[:, i, 2, :],
+                    in_=qkv[:, i, 2 * HEAD : ROT],
+                    func=ACT.Square,
+                    scale=1.0 / math.sqrt(HEAD),
+                    accum_out=mean_sq[:, i, 2:3],
+                )
+
+        def sum_q(g):
+            nc.vector.tensor_reduce(
+                out=live["mean_sq", g][:, :, 0:2],
+                in_=live["squares", g][:, :, 0:2, :],
+                axis=AXIS.X,
+                op=ALU.add,
+            )
+
+        def invert(g):
             inv_rms = work.tile([P, GROUP, NORMED], F32, name="inv_rms")
             live["inv_rms", g] = inv_rms
             nc.scalar.activation(
-                out=inv_rms[:], in_=mean_sq[:], func=ACT.Abs_reciprocal_sqrt, bias=eps[:, 0:1], scale=1.0
+                out=inv_rms[:],
+                in_=live["mean_sq", g][:],
+                func=ACT.Abs_reciprocal_sqrt,
+                bias=eps[:, 0:1],
+                scale=1.0,
             )
 
         def store_if_full(hbm, staged, g):
@@ -214,7 +237,7 @@ def tile_attention_pa_t_kernel(
 
         def copy_v(g):
             v_stage, rows = chunk_tile("v_stage", g, [P, CHUNK, HEAD])
-            nc.vector.tensor_copy(out=v_stage[:, rows, :], in_=live["qkv", g][:, :, ROT:QKV])
+            nc.scalar.copy(out=v_stage[:, rows, :], in_=live["qkv", g][:, :, ROT:QKV])
             store_if_full(v_rows, v_stage, g)
 
         def rotate(g):
@@ -240,7 +263,7 @@ def tile_attention_pa_t_kernel(
 
         def norm_k(g):
             k_stage, rows = chunk_tile("k_stage", g, [P, CHUNK, HEAD])
-            nc.vector.tensor_tensor(
+            nc.gpsimd.tensor_tensor(
                 out=k_stage[:, rows, :],
                 in0=live["rotated", g][:, :, 2 * HEAD : ROT],
                 in1=live["inv_rms", g][:, :, 2:3].to_broadcast([P, GROUP, HEAD]),
@@ -257,17 +280,17 @@ def tile_attention_pa_t_kernel(
                 stage_fn(g - 1)
                 stage_fn(g)
 
-        for step in range(GROUPS + 5):
+        for step in range(GROUPS + 4):
             run(load_x, step + LOOKAHEAD)
             run(transpose_x, step)
             run(quantise_x, step - 1)
             run_pair(project, step - 1)
-            if 2 <= step + 1 < TABLE_PARTS:
-                build_tables(step + 1)
-            run(norm_k, step - 5)
+            run(invert, step - 4)
             run(rotate, step - 4)
             run(norm_q, step - 4)
-            run(statistics, step - 3)
+            run(norm_k, step - 4)
+            run(square, step - 3)
+            run(copy_v, step - 3)
             run(regroup_x, step)
             run(products, step - 3)
-            run(copy_v, step - 3)
+            run(sum_q, step - 3)

@@ -285,12 +285,12 @@ def tile_attention_pa_t_kernel(
             run(transpose_x, step)
             run(quantise_x, step - 1)
             run_pair(project, step - 1)
-            run(invert, step - 4)
             run(rotate, step - 4)
-            run(norm_q, step - 4)
-            run(norm_k, step - 4)
             run(square, step - 3)
             run(copy_v, step - 3)
+            run(invert, step - 4)
+            run(norm_q, step - 4)
+            run(norm_k, step - 4)
             run(regroup_x, step)
             run(products, step - 3)
             run(sum_q, step - 3)

@@ -30,6 +30,7 @@ GROUP = 4
 GROUPS = BATCH * POS // GROUP
 CHUNK = 2 * GROUP
 WORDS = DIM // 2
+K_SCALAR = 2
 LOOKAHEAD = 6
 TABLE_PARTS = 4
 
@@ -261,12 +262,24 @@ def tile_attention_pa_t_kernel(
             )
             store_if_full(q_rows, q_stage, g)
 
-        def norm_k(g):
+        def norm_k_scalar(g):
             k_stage, rows = chunk_tile("k_stage", g, [P, CHUNK, HEAD])
-            nc.gpsimd.tensor_tensor(
-                out=k_stage[:, rows, :],
-                in0=live["rotated", g][:, :, 2 * HEAD : ROT],
-                in1=live["inv_rms", g][:, :, 2:3].to_broadcast([P, GROUP, HEAD]),
+            for i in range(K_SCALAR):
+                nc.scalar.activation(
+                    out=k_stage[:, rows.start + i, :],
+                    in_=live["rotated", g][:, i, 2 * HEAD : ROT],
+                    func=ACT.Copy,
+                    scale=live["inv_rms", g][:, i, 2:3],
+                )
+
+        def norm_k_vector(g):
+            k_stage, rows = chunk_tile("k_stage", g, [P, CHUNK, HEAD])
+            nc.vector.tensor_tensor(
+                out=k_stage[:, rows.start + K_SCALAR : rows.stop, :],
+                in0=live["rotated", g][:, K_SCALAR:GROUP, 2 * HEAD : ROT],
+                in1=live["inv_rms", g][:, K_SCALAR:GROUP, 2:3].to_broadcast(
+                    [P, GROUP - K_SCALAR, HEAD]
+                ),
                 op=ALU.mult,
             )
             store_if_full(k_rows, k_stage, g)
@@ -290,7 +303,8 @@ def tile_attention_pa_t_kernel(
             run(copy_v, step - 3)
             run(invert, step - 4)
             run(norm_q, step - 4)
-            run(norm_k, step - 4)
             run(regroup_x, step)
+            run(norm_k_scalar, step - 4)
             run(products, step - 3)
             run(sum_q, step - 3)
+            run(norm_k_vector, step - 4)

@@ -62,9 +62,10 @@ def tile_attention_pa_t_kernel(
             live["x", g] = x_tile
             nc.sync.dma_start(out=x_tile[:], in_=x_rows[b, :, first : first + GROUP, :])
 
-        gain_raw = const.tile([P, NORMED, HEAD], BF16)
-        nc.sync.dma_start(out=gain_raw[:, 0, :], in_=q_norm_w.partition_broadcast(P))
-        nc.sync.dma_start(out=gain_raw[:, 2, :], in_=k_norm_w.partition_broadcast(P))
+        gain_rows = const.tile([P, 2 * HEAD], BF16)
+        nc.gpsimd.memset(gain_rows[:], 0.0)
+        nc.sync.dma_start(out=gain_rows[0:1, 0:HEAD], in_=q_norm_w.rearrange("(o c) -> o c", o=1))
+        nc.sync.dma_start(out=gain_rows[0:1, HEAD : 2 * HEAD], in_=k_norm_w.rearrange("(o c) -> o c", o=1))
         fc = const.tile([P, POS, PAIRS, 2], BF16)
         nc.sync.dma_start(out=fc[:], in_=freqs_cis.rearrange("(p t) j e -> p t j e", t=POS))
         load_x(0)
@@ -85,7 +86,15 @@ def tile_attention_pa_t_kernel(
         eps = const.tile([P, 1], F32)
         nc.vector.memset(eps[:], EPS)
 
-        nc.vector.tensor_copy(out=gain_raw[:, 1, :], in_=gain_raw[:, 0, :])
+        ones = const.tile([P, P], BF16)
+        nc.vector.memset(ones[:], 1.0)
+        spread = psum_qkv.tile([P, 2 * HEAD], F32, name="qkv")
+        nc.tensor.matmul(out=spread[:], lhsT=ones[:], rhs=gain_rows[:], start=True, stop=True)
+        gain_raw = const.tile([P, NORMED, HEAD], BF16)
+        nc.vector.tensor_copy(
+            out=gain_raw[:, 0:2, :], in_=spread[:, 0:HEAD].unsqueeze(1).to_broadcast([P, 2, HEAD])
+        )
+        nc.vector.tensor_copy(out=gain_raw[:, 2, :], in_=spread[:, HEAD : 2 * HEAD])
         gain_pairs = gain_raw[:].rearrange("p h (j e) -> p h j e", e=2)
         gain_minus = const.tile([P, NORMED, PAIRS], BF16)
         nc.vector.tensor_scalar_mul(out=gain_minus[:], in0=gain_pairs[:, :, :, 1], scalar1=-1.0)

@@ -30,7 +30,7 @@ GROUP = 4
 GROUPS = BATCH * POS // GROUP
 CHUNK = 2 * GROUP
 WORDS = DIM // 2
-K_SCALAR = 2
+K_SCALAR = 4
 LOOKAHEAD = 6
 TABLE_PARTS = 4
 
@@ -222,7 +222,11 @@ def tile_attention_pa_t_kernel(
             )
 
         def store_if_full(hbm, staged, g):
-            if g % 2 == 1:
+            if g >= GROUPS - 2:
+                b, first = divmod(g * GROUP, POS)
+                rows = slice(g % 2 * GROUP, (g % 2 + 1) * GROUP)
+                nc.sync.dma_start(out=hbm[b, :, first : first + GROUP, :], in_=staged[:, rows, :])
+            elif g % 2 == 1:
                 b, first = divmod((g - 1) * GROUP, POS)
                 nc.sync.dma_start(out=hbm[b, :, first : first + CHUNK, :], in_=staged[:])
 
@@ -263,7 +267,8 @@ def tile_attention_pa_t_kernel(
 
         def norm_q(g):
             q_stage, rows = chunk_tile("q_stage", g, [P, CHUNK, 2 * HEAD])
-            nc.gpsimd.tensor_tensor(
+            engine = nc.vector if g == GROUPS - 1 else nc.gpsimd
+            engine.tensor_tensor(
                 out=q_stage[:, rows, :].rearrange("p i (h c) -> p i h c", c=HEAD),
                 in0=live["rotated", g][:, :, 0 : 2 * HEAD].rearrange("p i (h c) -> p i h c", c=HEAD),
                 in1=live["inv_rms", g][:, :, 0:2].unsqueeze(3).to_broadcast([P, GROUP, 2, HEAD]),
@@ -281,16 +286,8 @@ def tile_attention_pa_t_kernel(
                     scale=live["inv_rms", g][:, i, 2:3],
                 )
 
-        def norm_k_vector(g):
+        def store_k(g):
             k_stage, rows = chunk_tile("k_stage", g, [P, CHUNK, HEAD])
-            nc.vector.tensor_tensor(
-                out=k_stage[:, rows.start + K_SCALAR : rows.stop, :],
-                in0=live["rotated", g][:, K_SCALAR:GROUP, 2 * HEAD : ROT],
-                in1=live["inv_rms", g][:, K_SCALAR:GROUP, 2:3].to_broadcast(
-                    [P, GROUP - K_SCALAR, HEAD]
-                ),
-                op=ALU.mult,
-            )
             store_if_full(k_rows, k_stage, g)
 
         def run(stage_fn, g):
@@ -302,18 +299,18 @@ def tile_attention_pa_t_kernel(
                 stage_fn(g - 1)
                 stage_fn(g)
 
-        for step in range(GROUPS + 4):
+        for step in range(GROUPS + 3):
             run(load_x, step + LOOKAHEAD)
             run(transpose_x, step)
             run(quantise_x, step - 1)
-            run_pair(project, step - 1)
-            run(rotate, step - 4)
-            run(square, step - 3)
-            run(copy_v, step - 3)
-            run(invert, step - 4)
-            run(norm_q, step - 4)
+            run(project, step - 1)
+            run(rotate, step - 3)
+            run(square, step - 2)
+            run(copy_v, step - 2)
+            run(invert, step - 3)
+            run(norm_q, step - 3)
             run(regroup_x, step)
-            run(norm_k_scalar, step - 4)
-            run(products, step - 3)
-            run(sum_q, step - 3)
-            run(norm_k_vector, step - 4)
+            run(norm_k_scalar, step - 3)
+            run(store_k, step - 3)
+            run(products, step - 2)
+            run(sum_q, step - 2)

@@ -30,9 +30,11 @@ GROUP = 4
 GROUPS = BATCH * POS // GROUP
 CHUNK = 2 * GROUP
 WORDS = DIM // 2
+SCALAR_SUMS_FROM = GROUPS
 K_SCALAR = 4
 LOOKAHEAD = 6
 TABLE_PARTS = 4
+PART = POS // TABLE_PARTS
 
 FLOPS = 2 * BATCH * SEQ * DIM * QKV
 
@@ -56,19 +58,27 @@ def tile_attention_pa_t_kernel(
 
         live = {}
 
-        def load_x(g):
+        def load_x(g, pieces=1):
             b, first = divmod(g * GROUP, POS)
             x_tile = x_pool.tile([P, GROUP, DIM], BF16, name="x_tile")
             live["x", g] = x_tile
-            nc.sync.dma_start(out=x_tile[:], in_=x_rows[b, :, first : first + GROUP, :])
+            count = GROUP // pieces
+            for i in range(0, GROUP, count):
+                nc.sync.dma_start(
+                    out=x_tile[:, i : i + count, :], in_=x_rows[b, :, first + i : first + i + count, :]
+                )
 
         gain_rows = const.tile([P, 2 * HEAD], BF16)
         nc.gpsimd.memset(gain_rows[:], 0.0)
         nc.sync.dma_start(out=gain_rows[0:1, 0:HEAD], in_=q_norm_w.rearrange("(o c) -> o c", o=1))
         nc.sync.dma_start(out=gain_rows[0:1, HEAD : 2 * HEAD], in_=k_norm_w.rearrange("(o c) -> o c", o=1))
-        fc = const.tile([P, POS, PAIRS, 2], BF16)
-        nc.sync.dma_start(out=fc[:], in_=freqs_cis.rearrange("(p t) j e -> p t j e", t=POS))
-        load_x(0)
+        fc_rows = freqs_cis.rearrange("(p t) j e -> p t j e", t=POS)
+        fc_first = const.tile([P, PART, PAIRS, 2], BF16)
+        nc.sync.dma_start(out=fc_first[:], in_=fc_rows[:, 0:PART])
+        load_x(0, pieces=2)
+        fc_rest = const.tile([P, POS - PART, PAIRS, 2], BF16)
+        nc.sync.dma_start(out=fc_rest[:], in_=fc_rows[:, PART:POS])
+        load_x(1)
         w_words = const.tile([P, 2 * QKV], U8, align_bytes=64)
         nc.sync.dma_start(out=w_words[:].bitcast(I32), in_=wqkv_words[0].bitcast(I32))
         w_scales = const.tile([P, QKV], U8, align_bytes=64)
@@ -78,7 +88,7 @@ def tile_attention_pa_t_kernel(
                 out=w_scales[32 * quad : 32 * quad + 4, :].bitcast(I32),
                 in_=wqkv_scales[0, 4 * quad : 4 * quad + 4, :].bitcast(I32),
             )
-        for g in range(1, LOOKAHEAD):
+        for g in range(2, LOOKAHEAD):
             load_x(g)
 
         ident = const.tile([P, P], F32)
@@ -98,15 +108,16 @@ def tile_attention_pa_t_kernel(
         gain_pairs = gain_raw[:].rearrange("p h (j e) -> p h j e", e=2)
         gain_minus = const.tile([P, NORMED, PAIRS], BF16)
         nc.vector.tensor_scalar_mul(out=gain_minus[:], in0=gain_pairs[:, :, :, 1], scalar1=-1.0)
-        table_a = const.tile([P, 2, POS, ROT_PAIRS], F32)
-        table_b = const.tile([P, 2, POS, ROT_PAIRS], F32)
+        tables = {}
 
         def build_tables(part, engine):
-            count = POS // TABLE_PARTS
-            first = part * count
-            shape = [P, count, NORMED, PAIRS]
-            fr = fc[:, first : first + count, :, 0].unsqueeze(2).to_broadcast(shape)
-            fi = fc[:, first : first + count, :, 1].unsqueeze(2).to_broadcast(shape)
+            table_a = const.tile([P, 2, PART, ROT_PAIRS], F32, name="table_a%d" % part)
+            table_b = const.tile([P, 2, PART, ROT_PAIRS], F32, name="table_b%d" % part)
+            tables[part] = (table_a, table_b)
+            shape = [P, PART, NORMED, PAIRS]
+            fc = fc_first[:] if part == 0 else fc_rest[:, (part - 1) * PART : part * PART]
+            fr = fc[:, :, :, 0].unsqueeze(2).to_broadcast(shape)
+            fi = fc[:, :, :, 1].unsqueeze(2).to_broadcast(shape)
             g_even = gain_pairs[:, :, :, 0].unsqueeze(1).to_broadcast(shape)
             g_odd = gain_pairs[:, :, :, 1].unsqueeze(1).to_broadcast(shape)
             g_minus = gain_minus[:].unsqueeze(1).to_broadcast(shape)
@@ -117,18 +128,13 @@ def tile_attention_pa_t_kernel(
                 (table_b, 1, fr, g_odd),
             ):
                 engine.tensor_tensor(
-                    out=table[:, which, first : first + count, :].rearrange(
-                        "p t (h j) -> p t h j", h=NORMED
-                    ),
+                    out=table[:, which, :, :].rearrange("p t (h j) -> p t h j", h=NORMED),
                     in0=f,
                     in1=g,
                     op=ALU.mult,
                 )
 
         build_tables(0, nc.vector)
-        build_tables(1, nc.vector)
-        build_tables(2, nc.gpsimd)
-        build_tables(3, nc.gpsimd)
 
         def transpose_x(g):
             words = live["x", g][:].bitcast(F32)
@@ -187,22 +193,26 @@ def tile_attention_pa_t_kernel(
             mean_sq = work.tile([P, GROUP, NORMED], F32, name="mean_sq")
             live["squares", g] = squares
             live["mean_sq", g] = mean_sq
-            nc.scalar.activation(
-                out=squares[:, :, 0:2, :],
-                in_=qkv[:, :, 0 : 2 * HEAD].rearrange("p i (h c) -> p i h c", c=HEAD),
-                func=ACT.Square,
-                scale=1.0 / math.sqrt(HEAD),
-            )
-            for i in range(GROUP):
+            if g < SCALAR_SUMS_FROM:
                 nc.scalar.activation(
-                    out=squares[:, i, 2, :],
-                    in_=qkv[:, i, 2 * HEAD : ROT],
+                    out=squares[:, :, 0:2, :],
+                    in_=qkv[:, :, 0 : 2 * HEAD].rearrange("p i (h c) -> p i h c", c=HEAD),
                     func=ACT.Square,
                     scale=1.0 / math.sqrt(HEAD),
-                    accum_out=mean_sq[:, i, 2:3],
                 )
+            for i in range(GROUP):
+                for h in range(2 if g < SCALAR_SUMS_FROM else 0, NORMED):
+                    nc.scalar.activation(
+                        out=squares[:, i, h, :],
+                        in_=qkv[:, i, h * HEAD : (h + 1) * HEAD],
+                        func=ACT.Square,
+                        scale=1.0 / math.sqrt(HEAD),
+                        accum_out=mean_sq[:, i, h : h + 1],
+                    )
 
         def sum_q(g):
+            if g >= SCALAR_SUMS_FROM:
+                return
             nc.vector.tensor_reduce(
                 out=live["mean_sq", g][:, :, 0:2],
                 in_=live["squares", g][:, :, 0:2, :],
@@ -231,7 +241,8 @@ def tile_attention_pa_t_kernel(
                 nc.sync.dma_start(out=hbm[b, :, first : first + CHUNK, :], in_=staged[:])
 
         def products(g):
-            first = g * GROUP % POS
+            part, first = divmod(g * GROUP % POS, PART)
+            table_a, table_b = tables[part]
             pairs = live["qkv", g][:, :, 0:ROT].rearrange("p i (n e) -> p i n e", e=2)
             prod = work.tile([P, 4, GROUP, ROT_PAIRS], F32, name="prod")
             live["prod", g] = prod
@@ -303,6 +314,8 @@ def tile_attention_pa_t_kernel(
             run(load_x, step + LOOKAHEAD)
             run(transpose_x, step)
             run(quantise_x, step - 1)
+            if 1 <= step < TABLE_PARTS:
+                build_tables(step, nc.vector)
             run(project, step - 1)
             run(rotate, step - 3)
             run(square, step - 2)

@@ -114,13 +114,13 @@ def tile_attention_pa_t_kernel(
             table_a = const.tile([P, 2, PART, ROT_PAIRS], F32, name="table_a%d" % part)
             table_b = const.tile([P, 2, PART, ROT_PAIRS], F32, name="table_b%d" % part)
             tables[part] = (table_a, table_b)
-            shape = [P, PART, NORMED, PAIRS]
+            shape = [P, PART, NORMED - 1, PAIRS]
             fc = fc_first[:] if part == 0 else fc_rest[:, (part - 1) * PART : part * PART]
             fr = fc[:, :, :, 0].unsqueeze(2).to_broadcast(shape)
             fi = fc[:, :, :, 1].unsqueeze(2).to_broadcast(shape)
-            g_even = gain_pairs[:, :, :, 0].unsqueeze(1).to_broadcast(shape)
-            g_odd = gain_pairs[:, :, :, 1].unsqueeze(1).to_broadcast(shape)
-            g_minus = gain_minus[:].unsqueeze(1).to_broadcast(shape)
+            g_even = gain_pairs[:, 1:NORMED, :, 0].unsqueeze(1).to_broadcast(shape)
+            g_odd = gain_pairs[:, 1:NORMED, :, 1].unsqueeze(1).to_broadcast(shape)
+            g_minus = gain_minus[:, 1:NORMED, :].unsqueeze(1).to_broadcast(shape)
             for table, which, f, g in (
                 (table_a, 0, fr, g_even),
                 (table_a, 1, fi, g_even),
@@ -128,13 +128,18 @@ def tile_attention_pa_t_kernel(
                 (table_b, 1, fr, g_odd),
             ):
                 engine.tensor_tensor(
-                    out=table[:, which, :, :].rearrange("p t (h j) -> p t h j", h=NORMED),
+                    out=table[:, which, :, PAIRS:ROT_PAIRS].rearrange(
+                        "p t (h j) -> p t h j", h=NORMED - 1
+                    ),
                     in0=f,
                     in1=g,
                     op=ALU.mult,
                 )
+            for table in (table_a, table_b):
+                engine.tensor_copy(out=table[:, :, :, 0:PAIRS], in_=table[:, :, :, PAIRS : 2 * PAIRS])
 
         build_tables(0, nc.vector)
+        build_tables(1, nc.vector)
 
         def transpose_x(g):
             words = live["x", g][:].bitcast(F32)
@@ -314,8 +319,8 @@ def tile_attention_pa_t_kernel(
             run(load_x, step + LOOKAHEAD)
             run(transpose_x, step)
             run(quantise_x, step - 1)
-            if 1 <= step < TABLE_PARTS:
-                build_tables(step, nc.vector)
+            if 2 <= step + 1 < TABLE_PARTS:
+                build_tables(step + 1, nc.vector)
             run(project, step - 1)
             run(rotate, step - 3)
             run(square, step - 2)

@@ -30,7 +30,10 @@ GROUP = 4
 GROUPS = BATCH * POS // GROUP
 CHUNK = 2 * GROUP
 WORDS = DIM // 2
-SCALAR_SUMS_FROM = GROUPS
+SUMMED = GROUPS - 4
+VECTORS = 2 * GROUP * NORMED
+FOLDS = HEAD // 4
+NORM_LAG = 7
 K_SCALAR = 4
 LOOKAHEAD = 6
 TABLE_PARTS = 4
@@ -47,8 +50,10 @@ def tile_attention_pa_t_kernel(
         const = ctx.enter_context(tc.tile_pool(name="const", bufs=1))
         x_pool = ctx.enter_context(tc.tile_pool(name="x_pool", bufs=LOOKAHEAD + 2))
         work = ctx.enter_context(tc.tile_pool(name="work", bufs=3))
+        late = ctx.enter_context(tc.tile_pool(name="late", bufs=NORM_LAG))
         psum_xt = ctx.enter_context(tc.psum_pool(name="psum_xt", bufs=4))
-        psum_qkv = ctx.enter_context(tc.psum_pool(name="psum_qkv", bufs=4))
+        psum_qkv = ctx.enter_context(tc.psum_pool(name="psum_qkv", bufs=2))
+        psum_sum = ctx.enter_context(tc.psum_pool(name="psum_sum", bufs=2))
         ctx.enter_context(tc.manual_schedule())
 
         x_rows = x.rearrange("b (p t) d -> b p t d", t=POS)
@@ -95,6 +100,22 @@ def tile_attention_pa_t_kernel(
         make_identity(nc, ident[:])
         eps = const.tile([P, 1], F32)
         nc.vector.memset(eps[:], EPS)
+        warm = const.tile([P, 1], F32)
+        nc.scalar.activation(
+            out=warm[:], in_=eps[:], func=ACT.Abs_reciprocal_sqrt, bias=eps[:, 0:1], scale=1.0
+        )
+        gather = const.tile([P, VECTORS], F32)
+        nc.vector.tensor_reduce(
+            out=gather[:],
+            in_=ident[:, 0 : 4 * VECTORS].rearrange("p (r v) -> p v r", r=4),
+            axis=AXIS.X,
+            op=ALU.add,
+        )
+        chunk_squares = []
+        for i in range(2):
+            sq = const.tile([P, VECTORS * HEAD + P - 4 * VECTORS], F32, name="chunk_squares%d" % i)
+            nc.gpsimd.memset(sq[:, VECTORS * HEAD :], 0.0)
+            chunk_squares.append(sq)
 
         ones = const.tile([P, P], BF16)
         nc.vector.memset(ones[:], 1.0)
@@ -194,29 +215,40 @@ def tile_attention_pa_t_kernel(
 
         def square(g):
             qkv = live["qkv", g]
+            if g < SUMMED:
+                m, half = divmod(g, 2)
+                size = GROUP * NORMED
+                by_vector = chunk_squares[m % 2][:, 0 : VECTORS * HEAD].rearrange("p (c v) -> p c v", v=VECTORS)
+                nc.scalar.activation(
+                    out=by_vector[:, :, half * size : (half + 1) * size].rearrange(
+                        "p c (h i) -> p h c i", i=GROUP
+                    ),
+                    in_=qkv[:, :, 0:ROT].rearrange("p i (h c) -> p h c i", c=HEAD),
+                    func=ACT.Square,
+                    scale=1.0 / math.sqrt(HEAD),
+                )
+                return
             squares = work.tile([P, GROUP, NORMED, HEAD], F32, name="squares")
             mean_sq = work.tile([P, GROUP, NORMED], F32, name="mean_sq")
             live["squares", g] = squares
             live["mean_sq", g] = mean_sq
-            if g < SCALAR_SUMS_FROM:
+            nc.scalar.activation(
+                out=squares[:, :, 0:2, :],
+                in_=qkv[:, :, 0 : 2 * HEAD].rearrange("p i (h c) -> p i h c", c=HEAD),
+                func=ACT.Square,
+                scale=1.0 / math.sqrt(HEAD),
+            )
+            for i in range(GROUP):
                 nc.scalar.activation(
-                    out=squares[:, :, 0:2, :],
-                    in_=qkv[:, :, 0 : 2 * HEAD].rearrange("p i (h c) -> p i h c", c=HEAD),
+                    out=squares[:, i, 2, :],
+                    in_=qkv[:, i, 2 * HEAD : ROT],
                     func=ACT.Square,
                     scale=1.0 / math.sqrt(HEAD),
+                    accum_out=mean_sq[:, i, 2:3],
                 )
-            for i in range(GROUP):
-                for h in range(2 if g < SCALAR_SUMS_FROM else 0, NORMED):
-                    nc.scalar.activation(
-                        out=squares[:, i, h, :],
-                        in_=qkv[:, i, h * HEAD : (h + 1) * HEAD],
-                        func=ACT.Square,
-                        scale=1.0 / math.sqrt(HEAD),
-                        accum_out=mean_sq[:, i, h : h + 1],
-                    )
 
         def sum_q(g):
-            if g >= SCALAR_SUMS_FROM:
+            if g < SUMMED:
                 return
             nc.vector.tensor_reduce(
                 out=live["mean_sq", g][:, :, 0:2],
@@ -225,9 +257,46 @@ def tile_attention_pa_t_kernel(
                 op=ALU.add,
             )
 
+        def fold(m, first, last):
+            if first == 0:
+                live["fold", m] = psum_sum.tile([P, P], F32, name="sums")
+            for c in range(first, last):
+                nc.tensor.matmul(
+                    out=live["fold", m][:],
+                    lhsT=chunk_squares[m % 2][:, 4 * VECTORS * c : 4 * VECTORS * c + P],
+                    rhs=ident[:],
+                    is_transpose=True,
+                    start=c == 0,
+                    stop=c == FOLDS - 1,
+                )
+
+        def copy_fold(m):
+            folded = work.tile([P, P], F32, name="folded")
+            live["folded", m] = folded
+            nc.scalar.copy(out=folded[:], in_=live["fold", m][:])
+
+        def gather_sums(m):
+            sums = psum_sum.tile([P, VECTORS], F32, name="sums")
+            live["sums", m] = sums
+            nc.tensor.matmul(out=sums[:], lhsT=live["folded", m][:], rhs=gather[:], start=True, stop=True)
+
+        def invert_chunk(m):
+            inv_rms = late.tile([P, 2, NORMED, GROUP], F32, name="inv_rms2")
+            live["inv_rms", 2 * m] = inv_rms[:, 0].rearrange("p h i -> p i h")
+            live["inv_rms", 2 * m + 1] = inv_rms[:, 1].rearrange("p h i -> p i h")
+            nc.scalar.activation(
+                out=inv_rms[:].rearrange("p g h i -> p (g h i)"),
+                in_=live["sums", m][:],
+                func=ACT.Abs_reciprocal_sqrt,
+                bias=eps[:, 0:1],
+                scale=1.0,
+            )
+
         def invert(g):
+            if g < SUMMED:
+                return
             inv_rms = work.tile([P, GROUP, NORMED], F32, name="inv_rms")
-            live["inv_rms", g] = inv_rms
+            live["inv_rms", g] = inv_rms[:]
             nc.scalar.activation(
                 out=inv_rms[:],
                 in_=live["mean_sq", g][:],
@@ -249,7 +318,7 @@ def tile_attention_pa_t_kernel(
             part, first = divmod(g * GROUP % POS, PART)
             table_a, table_b = tables[part]
             pairs = live["qkv", g][:, :, 0:ROT].rearrange("p i (n e) -> p i n e", e=2)
-            prod = work.tile([P, 4, GROUP, ROT_PAIRS], F32, name="prod")
+            prod = late.tile([P, 4, GROUP, ROT_PAIRS], F32, name="prod")
             live["prod", g] = prod
             shape = [P, 2, GROUP, ROT_PAIRS]
             nc.vector.tensor_tensor(
@@ -283,7 +352,7 @@ def tile_attention_pa_t_kernel(
 
         def norm_q(g):
             q_stage, rows = chunk_tile("q_stage", g, [P, CHUNK, 2 * HEAD])
-            engine = nc.vector if g == GROUPS - 1 else nc.gpsimd
+            engine = nc.vector if g >= SUMMED else nc.gpsimd
             engine.tensor_tensor(
                 out=q_stage[:, rows, :].rearrange("p i (h c) -> p i h c", c=HEAD),
                 in0=live["rotated", g][:, :, 0 : 2 * HEAD].rearrange("p i (h c) -> p i h c", c=HEAD),
@@ -310,25 +379,36 @@ def tile_attention_pa_t_kernel(
             if 0 <= g < GROUPS:
                 stage_fn(g)
 
-        def run_pair(stage_fn, g):
-            if 0 <= g < GROUPS and g % 2 == 1:
-                stage_fn(g - 1)
-                stage_fn(g)
+        def run_chunk(stage_fn, g, *rest):
+            if 0 <= g < SUMMED and g % 2 == 1:
+                stage_fn(g // 2, *rest)
 
+        def norm_group(step):
+            return [g for g in range(GROUPS) if g + (NORM_LAG if g < SUMMED else 3) == step]
+
+        transpose_x(0)
         for step in range(GROUPS + 3):
             run(load_x, step + LOOKAHEAD)
-            run(transpose_x, step)
+            run(transpose_x, step + 1)
+            run_chunk(gather_sums, step - 5)
+            run_chunk(fold, step - 3, 0, FOLDS // 2)
+            run_chunk(fold, step - 4, FOLDS // 2, FOLDS)
             run(quantise_x, step - 1)
             if 2 <= step + 1 < TABLE_PARTS:
                 build_tables(step + 1, nc.vector)
             run(project, step - 1)
-            run(rotate, step - 3)
+            for g in norm_group(step):
+                rotate(g)
             run(square, step - 2)
             run(copy_v, step - 2)
             run(invert, step - 3)
-            run(norm_q, step - 3)
+            for g in norm_group(step):
+                norm_q(g)
             run(regroup_x, step)
-            run(norm_k_scalar, step - 3)
-            run(store_k, step - 3)
+            run_chunk(invert_chunk, step - 5)
+            run_chunk(copy_fold, step - 4)
+            for g in norm_group(step):
+                norm_k_scalar(g)
+                store_k(g)
             run(products, step - 2)
             run(sum_q, step - 2)

@@ -32,7 +32,8 @@ CHUNK = 2 * GROUP
 WORDS = DIM // 2
 SUMMED = GROUPS - 4
 VECTORS = 2 * GROUP * NORMED
-FOLDS = HEAD // 4
+CLASSES = P // VECTORS
+FOLDS = -(-HEAD // CLASSES)
 NORM_LAG = 7
 K_SCALAR = 4
 LOOKAHEAD = 6
@@ -73,6 +74,14 @@ def tile_attention_pa_t_kernel(
                     out=x_tile[:, i : i + count, :], in_=x_rows[b, :, first + i : first + i + count, :]
                 )
 
+        w_scales = const.tile([P, 2, QKV], U8, align_bytes=64)
+        nc.vector.memset(w_scales[:].bitcast(I32), 0)
+        w_passes = const.tile([P, 2 * (2 * QKV + 1)], U8, align_bytes=64)
+        nc.vector.memset(w_passes[:], 0)
+        w_words = const.tile([P, 2 * QKV], U8)
+        nc.sync.dma_start(out=w_words[:].bitcast(I32), in_=wqkv_words[0].bitcast(I32))
+        w_bytes = const.tile([P, 2, QKV], U8)
+        nc.vector.tensor_copy(out=w_bytes[:], in_=w_words[:].rearrange("p (n b) -> p b n", b=2))
         gain_rows = const.tile([P, 2 * HEAD], BF16)
         nc.gpsimd.memset(gain_rows[:], 0.0)
         nc.sync.dma_start(out=gain_rows[0:1, 0:HEAD], in_=q_norm_w.rearrange("(o c) -> o c", o=1))
@@ -81,17 +90,20 @@ def tile_attention_pa_t_kernel(
         fc_first = const.tile([P, PART, PAIRS, 2], BF16)
         nc.sync.dma_start(out=fc_first[:], in_=fc_rows[:, 0:PART])
         load_x(0, pieces=2)
+        w_halves = const.tile([P, 2, QKV], U8)
+        for u in range(2):
+            for b in range(2):
+                nc.sync.dma_start(
+                    out=w_halves[b:P:2, u, :].bitcast(I32),
+                    in_=w_bytes[64 * u : 64 * u + 64, b, :].bitcast(I32),
+                )
         fc_rest = const.tile([P, POS - PART, PAIRS, 2], BF16)
         nc.sync.dma_start(out=fc_rest[:], in_=fc_rows[:, PART:POS])
         load_x(1)
-        w_words = const.tile([P, 2 * QKV], U8, align_bytes=64)
-        nc.sync.dma_start(out=w_words[:].bitcast(I32), in_=wqkv_words[0].bitcast(I32))
-        w_scales = const.tile([P, QKV], U8, align_bytes=64)
-        nc.vector.memset(w_scales[:].bitcast(I32), 0)
-        for quad in range(4):
+        scale_rows = wqkv_scales[0].rearrange("(u q j) n -> q u j n", u=2, j=2)
+        for r in range(4):
             nc.sync.dma_start(
-                out=w_scales[32 * quad : 32 * quad + 4, :].bitcast(I32),
-                in_=wqkv_scales[0, 4 * quad : 4 * quad + 4, :].bitcast(I32),
+                out=w_scales[r:P:32, :, :].bitcast(I32), in_=scale_rows[:, :, r // 2, :].bitcast(I32)
             )
         for g in range(2, LOOKAHEAD):
             load_x(g)
@@ -107,13 +119,13 @@ def tile_attention_pa_t_kernel(
         gather = const.tile([P, VECTORS], F32)
         nc.vector.tensor_reduce(
             out=gather[:],
-            in_=ident[:, 0 : 4 * VECTORS].rearrange("p (r v) -> p v r", r=4),
+            in_=ident[:, 0 : CLASSES * VECTORS].rearrange("p (r v) -> p v r", r=CLASSES),
             axis=AXIS.X,
             op=ALU.add,
         )
         chunk_squares = []
         for i in range(2):
-            sq = const.tile([P, VECTORS * HEAD + P - 4 * VECTORS], F32, name="chunk_squares%d" % i)
+            sq = const.tile([P, (FOLDS - 1) * CLASSES * VECTORS + P], F32, name="chunk_squares%d" % i)
             nc.gpsimd.memset(sq[:, VECTORS * HEAD :], 0.0)
             chunk_squares.append(sq)
 
@@ -162,6 +174,10 @@ def tile_attention_pa_t_kernel(
         build_tables(0, nc.vector)
         build_tables(1, nc.vector)
 
+        nc.vector.tensor_copy(
+            out=w_passes[:].rearrange("p (u m) -> p u m", u=2)[:, :, 0 : 2 * QKV : 2], in_=w_halves[:]
+        )
+
         def transpose_x(g):
             words = live["x", g][:].bitcast(F32)
             for half in range(2):
@@ -170,7 +186,7 @@ def tile_attention_pa_t_kernel(
                 for i in range(2):
                     for u in range(2):
                         nc.tensor.transpose(
-                            xt[:, i, u, :], words[:, 2 * half + i, u:WORDS:2], ident[:]
+                            xt[:, i, u, :], words[:, 2 * half + i, u * P : (u + 1) * P], ident[:]
                         )
 
         def regroup_x(g):
@@ -197,15 +213,16 @@ def tile_attention_pa_t_kernel(
             live["qkv", g] = qkv
             for i in range(GROUP):
                 tokens = slice(i * P, (i + 1) * P)
-                nc.tensor.matmul_mx(
-                    out=qkv[:, i, :],
-                    lhsT=codes[:, tokens].bitcast(FP8X4),
-                    lhsT_scale=planes[:, tokens],
-                    rhs=w_words[:].bitcast(FP4X4),
-                    rhs_scale=w_scales[:],
-                    start=True,
-                    stop=True,
-                )
+                for u in range(2):
+                    nc.tensor.matmul_mx(
+                        out=qkv[:, i, :],
+                        lhsT=codes[:, tokens].bitcast(FP8X4),
+                        lhsT_scale=planes[:, tokens],
+                        rhs=w_passes[:, 2 * QKV * u : 2 * QKV * (u + 1)].bitcast(FP4X4),
+                        rhs_scale=w_scales[:, u, :],
+                        start=u == 0,
+                        stop=u == 1,
+                    )
 
         def chunk_tile(name, g, shape):
             c, first = divmod(g * GROUP, CHUNK)
@@ -263,7 +280,7 @@ def tile_attention_pa_t_kernel(
             for c in range(first, last):
                 nc.tensor.matmul(
                     out=live["fold", m][:],
-                    lhsT=chunk_squares[m % 2][:, 4 * VECTORS * c : 4 * VECTORS * c + P],
+                    lhsT=chunk_squares[m % 2][:, CLASSES * VECTORS * c : CLASSES * VECTORS * c + P],
                     rhs=ident[:],
                     is_transpose=True,
                     start=c == 0,

@@ -30,11 +30,13 @@ GROUP = 4
 GROUPS = BATCH * POS // GROUP
 CHUNK = 2 * GROUP
 WORDS = DIM // 2
-SUMMED = GROUPS - 4
+SUMMED = GROUPS - 2
 VECTORS = 2 * GROUP * NORMED
 CLASSES = P // VECTORS
 FOLDS = -(-HEAD // CLASSES)
-NORM_LAG = 7
+FOLD_LAG = 3
+VECTOR_NORMS = GROUPS - 3
+NORM_LAG = 6
 K_SCALAR = 4
 LOOKAHEAD = 6
 TABLE_PARTS = 4
@@ -90,13 +92,6 @@ def tile_attention_pa_t_kernel(
         fc_first = const.tile([P, PART, PAIRS, 2], BF16)
         nc.sync.dma_start(out=fc_first[:], in_=fc_rows[:, 0:PART])
         load_x(0, pieces=2)
-        w_halves = const.tile([P, 2, QKV], U8)
-        for u in range(2):
-            for b in range(2):
-                nc.sync.dma_start(
-                    out=w_halves[b:P:2, u, :].bitcast(I32),
-                    in_=w_bytes[64 * u : 64 * u + 64, b, :].bitcast(I32),
-                )
         fc_rest = const.tile([P, POS - PART, PAIRS, 2], BF16)
         nc.sync.dma_start(out=fc_rest[:], in_=fc_rows[:, PART:POS])
         load_x(1)
@@ -105,7 +100,15 @@ def tile_attention_pa_t_kernel(
             nc.sync.dma_start(
                 out=w_scales[r:P:32, :, :].bitcast(I32), in_=scale_rows[:, :, r // 2, :].bitcast(I32)
             )
-        for g in range(2, LOOKAHEAD):
+        load_x(2)
+        w_halves = const.tile([P, 2, QKV], U8)
+        for u in range(2):
+            for b in range(2):
+                nc.sync.dma_start(
+                    out=w_halves[b:P:2, u, :].bitcast(I32),
+                    in_=w_bytes[64 * u : 64 * u + 64, b, :].bitcast(I32),
+                )
+        for g in range(3, LOOKAHEAD):
             load_x(g)
 
         ident = const.tile([P, P], F32)
@@ -246,7 +249,7 @@ def tile_attention_pa_t_kernel(
                 )
                 return
             squares = work.tile([P, GROUP, NORMED, HEAD], F32, name="squares")
-            mean_sq = work.tile([P, GROUP, NORMED], F32, name="mean_sq")
+            mean_sq = work.tile([P, NORMED, GROUP], F32, name="mean_sq")
             live["squares", g] = squares
             live["mean_sq", g] = mean_sq
             nc.scalar.activation(
@@ -261,15 +264,15 @@ def tile_attention_pa_t_kernel(
                     in_=qkv[:, i, 2 * HEAD : ROT],
                     func=ACT.Square,
                     scale=1.0 / math.sqrt(HEAD),
-                    accum_out=mean_sq[:, i, 2:3],
+                    accum_out=mean_sq[:, 2, i : i + 1],
                 )
 
         def sum_q(g):
             if g < SUMMED:
                 return
             nc.vector.tensor_reduce(
-                out=live["mean_sq", g][:, :, 0:2],
-                in_=live["squares", g][:, :, 0:2, :],
+                out=live["mean_sq", g][:, 0:2, :],
+                in_=live["squares", g][:, :, 0:2, :].rearrange("p i h c -> p h i c"),
                 axis=AXIS.X,
                 op=ALU.add,
             )
@@ -297,26 +300,17 @@ def tile_attention_pa_t_kernel(
             live["sums", m] = sums
             nc.tensor.matmul(out=sums[:], lhsT=live["folded", m][:], rhs=gather[:], start=True, stop=True)
 
-        def invert_chunk(m):
-            inv_rms = late.tile([P, 2, NORMED, GROUP], F32, name="inv_rms2")
-            live["inv_rms", 2 * m] = inv_rms[:, 0].rearrange("p h i -> p i h")
-            live["inv_rms", 2 * m + 1] = inv_rms[:, 1].rearrange("p h i -> p i h")
-            nc.scalar.activation(
-                out=inv_rms[:].rearrange("p g h i -> p (g h i)"),
-                in_=live["sums", m][:],
-                func=ACT.Abs_reciprocal_sqrt,
-                bias=eps[:, 0:1],
-                scale=1.0,
-            )
-
         def invert(g):
+            inv_rms = work.tile([P, NORMED, GROUP], F32, name="inv_rms")
+            live["inv_rms", g] = inv_rms[:].rearrange("p h i -> p i h")
             if g < SUMMED:
-                return
-            inv_rms = work.tile([P, GROUP, NORMED], F32, name="inv_rms")
-            live["inv_rms", g] = inv_rms[:]
+                m, half = divmod(g, 2)
+                mean_sq = live["sums", m][:, half * GROUP * NORMED : (half + 1) * GROUP * NORMED]
+            else:
+                mean_sq = live["mean_sq", g][:].rearrange("p h i -> p (h i)")
             nc.scalar.activation(
-                out=inv_rms[:],
-                in_=live["mean_sq", g][:],
+                out=inv_rms[:].rearrange("p h i -> p (h i)"),
+                in_=mean_sq,
                 func=ACT.Abs_reciprocal_sqrt,
                 bias=eps[:, 0:1],
                 scale=1.0,
@@ -335,7 +329,7 @@ def tile_attention_pa_t_kernel(
             part, first = divmod(g * GROUP % POS, PART)
             table_a, table_b = tables[part]
             pairs = live["qkv", g][:, :, 0:ROT].rearrange("p i (n e) -> p i n e", e=2)
-            prod = late.tile([P, 4, GROUP, ROT_PAIRS], F32, name="prod")
+            prod = work.tile([P, 4, GROUP, ROT_PAIRS], F32, name="prod")
             live["prod", g] = prod
             shape = [P, 2, GROUP, ROT_PAIRS]
             nc.vector.tensor_tensor(
@@ -353,12 +347,15 @@ def tile_attention_pa_t_kernel(
 
         def copy_v(g):
             v_stage, rows = chunk_tile("v_stage", g, [P, CHUNK, HEAD])
-            nc.scalar.copy(out=v_stage[:, rows, :], in_=live["qkv", g][:, :, ROT:QKV])
+            if g % 2 == 1 and g < SUMMED:
+                nc.vector.tensor_copy(out=v_stage[:, rows, :], in_=live["qkv", g][:, :, ROT:QKV])
+            else:
+                nc.scalar.copy(out=v_stage[:, rows, :], in_=live["qkv", g][:, :, ROT:QKV])
             store_if_full(v_rows, v_stage, g)
 
         def rotate(g):
             prod = live["prod", g]
-            rotated = work.tile([P, GROUP, ROT], F32, name="rotated")
+            rotated = late.tile([P, GROUP, ROT], F32, name="rotated")
             live["rotated", g] = rotated
             nc.vector.tensor_tensor(
                 out=rotated[:].rearrange("p i (n e) -> p (i n) e", e=2),
@@ -369,7 +366,7 @@ def tile_attention_pa_t_kernel(
 
         def norm_q(g):
             q_stage, rows = chunk_tile("q_stage", g, [P, CHUNK, 2 * HEAD])
-            engine = nc.vector if g >= SUMMED else nc.gpsimd
+            engine = nc.vector if g >= VECTOR_NORMS else nc.gpsimd
             engine.tensor_tensor(
                 out=q_stage[:, rows, :].rearrange("p i (h c) -> p i h c", c=HEAD),
                 in0=live["rotated", g][:, :, 0 : 2 * HEAD].rearrange("p i (h c) -> p i h c", c=HEAD),
@@ -401,31 +398,33 @@ def tile_attention_pa_t_kernel(
                 stage_fn(g // 2, *rest)
 
         def norm_group(step):
-            return [g for g in range(GROUPS) if g + (NORM_LAG if g < SUMMED else 3) == step]
+            return [g for g in range(GROUPS) if min(g + (NORM_LAG if g < SUMMED else 3), GROUPS + 2) == step]
 
         transpose_x(0)
         for step in range(GROUPS + 3):
             run(load_x, step + LOOKAHEAD)
             run(transpose_x, step + 1)
-            run_chunk(gather_sums, step - 5)
-            run_chunk(fold, step - 3, 0, FOLDS // 2)
-            run_chunk(fold, step - 4, FOLDS // 2, FOLDS)
+            run_chunk(gather_sums, step - FOLD_LAG - 1)
+            run_chunk(fold, step - FOLD_LAG, 0, FOLDS)
             run(quantise_x, step - 1)
             if 2 <= step + 1 < TABLE_PARTS:
                 build_tables(step + 1, nc.vector)
             run(project, step - 1)
-            for g in norm_group(step):
-                rotate(g)
+            run(rotate, step - 3)
             run(square, step - 2)
             run(copy_v, step - 2)
-            run(invert, step - 3)
             for g in norm_group(step):
-                norm_q(g)
+                invert(g)
+            for g in norm_group(step):
+                if g < VECTOR_NORMS:
+                    norm_q(g)
             run(regroup_x, step)
-            run_chunk(invert_chunk, step - 5)
-            run_chunk(copy_fold, step - 4)
+            run_chunk(copy_fold, step - FOLD_LAG)
             for g in norm_group(step):
                 norm_k_scalar(g)
                 store_k(g)
             run(products, step - 2)
             run(sum_q, step - 2)
+            for g in norm_group(step):
+                if g >= VECTOR_NORMS:
+                    norm_q(g)

@@ -35,7 +35,7 @@ VECTORS = 2 * GROUP * NORMED
 CLASSES = P // VECTORS
 FOLDS = -(-HEAD // CLASSES)
 FOLD_LAG = 3
-VECTOR_NORMS = GROUPS - 3
+VECTOR_NORMS = GROUPS - 4
 NORM_LAG = 6
 K_SCALAR = 4
 LOOKAHEAD = 6
@@ -76,6 +76,14 @@ def tile_attention_pa_t_kernel(
                     out=x_tile[:, i : i + count, :], in_=x_rows[b, :, first + i : first + i + count, :]
                 )
 
+        gain_rows = const.tile([P, 2 * HEAD], BF16)
+        nc.gpsimd.memset(gain_rows[:], 0.0)
+        nc.sync.dma_start(out=gain_rows[0:1, 0:HEAD], in_=q_norm_w.rearrange("(o c) -> o c", o=1))
+        nc.sync.dma_start(out=gain_rows[0:1, HEAD : 2 * HEAD], in_=k_norm_w.rearrange("(o c) -> o c", o=1))
+        ones = const.tile([P, P], BF16)
+        nc.vector.memset(ones[:], 1.0)
+        eps = const.tile([P, 1], F32)
+        nc.vector.memset(eps[:], EPS)
         w_scales = const.tile([P, 2, QKV], U8, align_bytes=64)
         nc.vector.memset(w_scales[:].bitcast(I32), 0)
         w_passes = const.tile([P, 2 * (2 * QKV + 1)], U8, align_bytes=64)
@@ -84,10 +92,6 @@ def tile_attention_pa_t_kernel(
         nc.sync.dma_start(out=w_words[:].bitcast(I32), in_=wqkv_words[0].bitcast(I32))
         w_bytes = const.tile([P, 2, QKV], U8)
         nc.vector.tensor_copy(out=w_bytes[:], in_=w_words[:].rearrange("p (n b) -> p b n", b=2))
-        gain_rows = const.tile([P, 2 * HEAD], BF16)
-        nc.gpsimd.memset(gain_rows[:], 0.0)
-        nc.sync.dma_start(out=gain_rows[0:1, 0:HEAD], in_=q_norm_w.rearrange("(o c) -> o c", o=1))
-        nc.sync.dma_start(out=gain_rows[0:1, HEAD : 2 * HEAD], in_=k_norm_w.rearrange("(o c) -> o c", o=1))
         fc_rows = freqs_cis.rearrange("(p t) j e -> p t j e", t=POS)
         fc_first = const.tile([P, PART, PAIRS, 2], BF16)
         nc.sync.dma_start(out=fc_first[:], in_=fc_rows[:, 0:PART])
@@ -113,18 +117,9 @@ def tile_attention_pa_t_kernel(
 
         ident = const.tile([P, P], F32)
         make_identity(nc, ident[:])
-        eps = const.tile([P, 1], F32)
-        nc.vector.memset(eps[:], EPS)
         warm = const.tile([P, 1], F32)
         nc.scalar.activation(
             out=warm[:], in_=eps[:], func=ACT.Abs_reciprocal_sqrt, bias=eps[:, 0:1], scale=1.0
-        )
-        gather = const.tile([P, VECTORS], F32)
-        nc.vector.tensor_reduce(
-            out=gather[:],
-            in_=ident[:, 0 : CLASSES * VECTORS].rearrange("p (r v) -> p v r", r=CLASSES),
-            axis=AXIS.X,
-            op=ALU.add,
         )
         chunk_squares = []
         for i in range(2):
@@ -132,8 +127,6 @@ def tile_attention_pa_t_kernel(
             nc.gpsimd.memset(sq[:, VECTORS * HEAD :], 0.0)
             chunk_squares.append(sq)
 
-        ones = const.tile([P, P], BF16)
-        nc.vector.memset(ones[:], 1.0)
         spread = psum_qkv.tile([P, 2 * HEAD], F32, name="qkv")
         nc.tensor.matmul(out=spread[:], lhsT=ones[:], rhs=gain_rows[:], start=True, stop=True)
         gain_raw = const.tile([P, NORMED, HEAD], BF16)
@@ -172,14 +165,29 @@ def tile_attention_pa_t_kernel(
                     op=ALU.mult,
                 )
             for table in (table_a, table_b):
-                engine.tensor_copy(out=table[:, :, :, 0:PAIRS], in_=table[:, :, :, PAIRS : 2 * PAIRS])
+                out, in_ = table[:, :, :, 0:PAIRS], table[:, :, :, PAIRS : 2 * PAIRS]
+                if part < 2:
+                    engine.tensor_copy(out=out, in_=in_)
+                else:
+                    nc.sync.dma_start(out=out, in_=in_)
 
         build_tables(0, nc.vector)
         build_tables(1, nc.vector)
 
-        nc.vector.tensor_copy(
-            out=w_passes[:].rearrange("p (u m) -> p u m", u=2)[:, :, 0 : 2 * QKV : 2], in_=w_halves[:]
-        )
+        def expand_w():
+            nc.vector.tensor_copy(
+                out=w_passes[:].rearrange("p (u m) -> p u m", u=2)[:, :, 0 : 2 * QKV : 2], in_=w_halves[:]
+            )
+
+        gather = const.tile([P, VECTORS], F32)
+
+        def make_gather():
+            nc.vector.tensor_reduce(
+                out=gather[:],
+                in_=ident[:, 0 : CLASSES * VECTORS].rearrange("p (r v) -> p v r", r=CLASSES),
+                axis=AXIS.X,
+                op=ALU.add,
+            )
 
         def transpose_x(g):
             words = live["x", g][:].bitcast(F32)
@@ -347,7 +355,7 @@ def tile_attention_pa_t_kernel(
 
         def copy_v(g):
             v_stage, rows = chunk_tile("v_stage", g, [P, CHUNK, HEAD])
-            if g % 2 == 1 and g < SUMMED:
+            if g % 2 == 1 and 4 < g < SUMMED:
                 nc.vector.tensor_copy(out=v_stage[:, rows, :], in_=live["qkv", g][:, :, ROT:QKV])
             else:
                 nc.scalar.copy(out=v_stage[:, rows, :], in_=live["qkv", g][:, :, ROT:QKV])
@@ -407,6 +415,10 @@ def tile_attention_pa_t_kernel(
             run_chunk(gather_sums, step - FOLD_LAG - 1)
             run_chunk(fold, step - FOLD_LAG, 0, FOLDS)
             run(quantise_x, step - 1)
+            if step == 1:
+                expand_w()
+            if step == 3:
+                make_gather()
             if 2 <= step + 1 < TABLE_PARTS:
                 build_tables(step + 1, nc.vector)
             run(project, step - 1)

@@ -37,6 +37,7 @@ FOLDS = -(-HEAD // CLASSES)
 FOLD_LAG = 3
 VECTOR_NORMS = GROUPS - 4
 NORM_LAG = 6
+Q_GPSIMD = 3
 K_SCALAR = 4
 LOOKAHEAD = 6
 TABLE_PARTS = 4
@@ -165,11 +166,7 @@ def tile_attention_pa_t_kernel(
                     op=ALU.mult,
                 )
             for table in (table_a, table_b):
-                out, in_ = table[:, :, :, 0:PAIRS], table[:, :, :, PAIRS : 2 * PAIRS]
-                if part < 2:
-                    engine.tensor_copy(out=out, in_=in_)
-                else:
-                    nc.sync.dma_start(out=out, in_=in_)
+                engine.tensor_copy(out=table[:, :, :, 0:PAIRS], in_=table[:, :, :, PAIRS : 2 * PAIRS])
 
         build_tables(0, nc.vector)
         build_tables(1, nc.vector)
@@ -179,11 +176,12 @@ def tile_attention_pa_t_kernel(
                 out=w_passes[:].rearrange("p (u m) -> p u m", u=2)[:, :, 0 : 2 * QKV : 2], in_=w_halves[:]
             )
 
-        gather = const.tile([P, VECTORS], F32)
+        gather = const.tile([P, P // 2], F32)
+        nc.gpsimd.memset(gather[:, VECTORS:], 0.0)
 
         def make_gather():
             nc.vector.tensor_reduce(
-                out=gather[:],
+                out=gather[:, 0:VECTORS],
                 in_=ident[:, 0 : CLASSES * VECTORS].rearrange("p (r v) -> p v r", r=CLASSES),
                 axis=AXIS.X,
                 op=ALU.add,
@@ -304,7 +302,7 @@ def tile_attention_pa_t_kernel(
             nc.scalar.copy(out=folded[:], in_=live["fold", m][:])
 
         def gather_sums(m):
-            sums = psum_sum.tile([P, VECTORS], F32, name="sums")
+            sums = psum_sum.tile([P, P // 2], F32, name="sums")
             live["sums", m] = sums
             nc.tensor.matmul(out=sums[:], lhsT=live["folded", m][:], rhs=gather[:], start=True, stop=True)
 
@@ -355,7 +353,7 @@ def tile_attention_pa_t_kernel(
 
         def copy_v(g):
             v_stage, rows = chunk_tile("v_stage", g, [P, CHUNK, HEAD])
-            if g % 2 == 1 and 4 < g < SUMMED:
+            if 4 < g < SUMMED:
                 nc.vector.tensor_copy(out=v_stage[:, rows, :], in_=live["qkv", g][:, :, ROT:QKV])
             else:
                 nc.scalar.copy(out=v_stage[:, rows, :], in_=live["qkv", g][:, :, ROT:QKV])
@@ -375,12 +373,25 @@ def tile_attention_pa_t_kernel(
         def norm_q(g):
             q_stage, rows = chunk_tile("q_stage", g, [P, CHUNK, 2 * HEAD])
             engine = nc.vector if g >= VECTOR_NORMS else nc.gpsimd
+            count = GROUP if g >= VECTOR_NORMS else Q_GPSIMD
             engine.tensor_tensor(
-                out=q_stage[:, rows, :].rearrange("p i (h c) -> p i h c", c=HEAD),
-                in0=live["rotated", g][:, :, 0 : 2 * HEAD].rearrange("p i (h c) -> p i h c", c=HEAD),
-                in1=live["inv_rms", g][:, :, 0:2].unsqueeze(3).to_broadcast([P, GROUP, 2, HEAD]),
+                out=q_stage[:, rows.start : rows.start + count, :].rearrange("p i (h c) -> p i h c", c=HEAD),
+                in0=live["rotated", g][:, 0:count, 0 : 2 * HEAD].rearrange("p i (h c) -> p i h c", c=HEAD),
+                in1=live["inv_rms", g][:, 0:count, 0:2].unsqueeze(3).to_broadcast([P, count, 2, HEAD]),
                 op=ALU.mult,
             )
+
+        def norm_q_scalar(g):
+            q_stage, rows = chunk_tile("q_stage", g, [P, CHUNK, 2 * HEAD])
+            if g < VECTOR_NORMS:
+                for i in range(Q_GPSIMD, GROUP):
+                    for h in range(2):
+                        nc.scalar.activation(
+                            out=q_stage[:, rows.start + i, h * HEAD : (h + 1) * HEAD],
+                            in_=live["rotated", g][:, i, h * HEAD : (h + 1) * HEAD],
+                            func=ACT.Copy,
+                            scale=live["inv_rms", g][:, i, h : h + 1],
+                        )
             store_if_full(q_rows, q_stage, g)
 
         def norm_k_scalar(g):
@@ -440,3 +451,4 @@ def tile_attention_pa_t_kernel(
             for g in norm_group(step):
                 if g >= VECTOR_NORMS:
                     norm_q(g)
+                norm_q_scalar(g)

@@ -81,14 +81,24 @@ def tile_attention_pa_t_kernel(
         nc.gpsimd.memset(gain_rows[:], 0.0)
         nc.sync.dma_start(out=gain_rows[0:1, 0:HEAD], in_=q_norm_w.rearrange("(o c) -> o c", o=1))
         nc.sync.dma_start(out=gain_rows[0:1, HEAD : 2 * HEAD], in_=k_norm_w.rearrange("(o c) -> o c", o=1))
-        ones = const.tile([P, P], BF16)
-        nc.vector.memset(ones[:], 1.0)
-        eps = const.tile([P, 1], F32)
-        nc.vector.memset(eps[:], EPS)
         w_scales = const.tile([P, 2, QKV], U8, align_bytes=64)
         nc.vector.memset(w_scales[:].bitcast(I32), 0)
         w_passes = const.tile([P, 2 * (2 * QKV + 1)], U8, align_bytes=64)
         nc.vector.memset(w_passes[:], 0)
+        ones = const.tile([P, P], BF16)
+        nc.vector.memset(ones[:], 1.0)
+        eps = const.tile([P, 1], F32)
+        nc.vector.memset(eps[:], EPS)
+        ident = const.tile([P, P], F32)
+        make_identity(nc, ident[:])
+        gather = const.tile([P, P // 2], F32)
+        nc.gpsimd.memset(gather[:, VECTORS:], 0.0)
+        nc.vector.tensor_reduce(
+            out=gather[:, 0:VECTORS],
+            in_=ident[:, 0 : CLASSES * VECTORS].rearrange("p (r v) -> p v r", r=CLASSES),
+            axis=AXIS.X,
+            op=ALU.add,
+        )
         w_words = const.tile([P, 2 * QKV], U8)
         nc.sync.dma_start(out=w_words[:].bitcast(I32), in_=wqkv_words[0].bitcast(I32))
         w_bytes = const.tile([P, 2, QKV], U8)
@@ -116,8 +126,6 @@ def tile_attention_pa_t_kernel(
         for g in range(3, LOOKAHEAD):
             load_x(g)
 
-        ident = const.tile([P, P], F32)
-        make_identity(nc, ident[:])
         warm = const.tile([P, 1], F32)
         nc.scalar.activation(
             out=warm[:], in_=eps[:], func=ACT.Abs_reciprocal_sqrt, bias=eps[:, 0:1], scale=1.0
@@ -174,17 +182,6 @@ def tile_attention_pa_t_kernel(
         def expand_w():
             nc.vector.tensor_copy(
                 out=w_passes[:].rearrange("p (u m) -> p u m", u=2)[:, :, 0 : 2 * QKV : 2], in_=w_halves[:]
-            )
-
-        gather = const.tile([P, P // 2], F32)
-        nc.gpsimd.memset(gather[:, VECTORS:], 0.0)
-
-        def make_gather():
-            nc.vector.tensor_reduce(
-                out=gather[:, 0:VECTORS],
-                in_=ident[:, 0 : CLASSES * VECTORS].rearrange("p (r v) -> p v r", r=CLASSES),
-                axis=AXIS.X,
-                op=ALU.add,
             )
 
         def transpose_x(g):
@@ -353,7 +350,7 @@ def tile_attention_pa_t_kernel(
 
         def copy_v(g):
             v_stage, rows = chunk_tile("v_stage", g, [P, CHUNK, HEAD])
-            if 4 < g < SUMMED:
+            if g % 2 == 1 and 8 < g < SUMMED:
                 nc.vector.tensor_copy(out=v_stage[:, rows, :], in_=live["qkv", g][:, :, ROT:QKV])
             else:
                 nc.scalar.copy(out=v_stage[:, rows, :], in_=live["qkv", g][:, :, ROT:QKV])
@@ -373,7 +370,7 @@ def tile_attention_pa_t_kernel(
         def norm_q(g):
             q_stage, rows = chunk_tile("q_stage", g, [P, CHUNK, 2 * HEAD])
             engine = nc.vector if g >= VECTOR_NORMS else nc.gpsimd
-            count = GROUP if g >= VECTOR_NORMS else Q_GPSIMD
+            count = Q_GPSIMD if g < VECTOR_NORMS and g % 2 == 0 else GROUP
             engine.tensor_tensor(
                 out=q_stage[:, rows.start : rows.start + count, :].rearrange("p i (h c) -> p i h c", c=HEAD),
                 in0=live["rotated", g][:, 0:count, 0 : 2 * HEAD].rearrange("p i (h c) -> p i h c", c=HEAD),
@@ -383,7 +380,7 @@ def tile_attention_pa_t_kernel(
 
         def norm_q_scalar(g):
             q_stage, rows = chunk_tile("q_stage", g, [P, CHUNK, 2 * HEAD])
-            if g < VECTOR_NORMS:
+            if g < VECTOR_NORMS and g % 2 == 0:
                 for i in range(Q_GPSIMD, GROUP):
                     for h in range(2):
                         nc.scalar.activation(
@@ -423,16 +420,14 @@ def tile_attention_pa_t_kernel(
         for step in range(GROUPS + 3):
             run(load_x, step + LOOKAHEAD)
             run(transpose_x, step + 1)
-            run_chunk(gather_sums, step - FOLD_LAG - 1)
             run_chunk(fold, step - FOLD_LAG, 0, FOLDS)
             run(quantise_x, step - 1)
             if step == 1:
                 expand_w()
-            if step == 3:
-                make_gather()
             if 2 <= step + 1 < TABLE_PARTS:
                 build_tables(step + 1, nc.vector)
             run(project, step - 1)
+            run_chunk(gather_sums, step - FOLD_LAG - 1)
             run(rotate, step - 3)
             run(square, step - 2)
             run(copy_v, step - 2)

from contextlib import ExitStack
import math

import concourse.mybir as mybir
from concourse.masks import make_identity

F32 = mybir.dt.float32
BF16 = mybir.dt.bfloat16
I32 = mybir.dt.int32
U32 = mybir.dt.uint32
U8 = mybir.dt.uint8
FP8X4 = mybir.dt.float8_e4m3fn_x4
FP4X4 = mybir.dt.float4_e2m1fn_x4
ACT = mybir.ActivationFunctionType
ALU = mybir.AluOpType
AXIS = mybir.AxisListType

P = 128
BATCH, SEQ, DIM = 4, 4096, 512
HEAD = 32
PAIRS = HEAD // 2
NORMED = 3
ROT = NORMED * HEAD
ROT_PAIRS = NORMED * PAIRS
QKV = ROT + HEAD
EPS = 1e-6

POS = SEQ // P
GROUP = 4
GROUPS = BATCH * POS // GROUP
CHUNK = 2 * GROUP
WORDS = DIM // 2
SUMMED = GROUPS - 2
VECTORS = 2 * GROUP * NORMED
CLASSES = P // VECTORS
FOLDS = -(-HEAD // CLASSES)
FOLD_LAG = 3
VECTOR_NORMS = GROUPS - 4
NORM_LAG = 6
Q_GPSIMD = 3
K_SCALAR = 4
LOOKAHEAD = 6
TABLE_PARTS = 4
PART = POS // TABLE_PARTS

FLOPS = 2 * BATCH * SEQ * DIM * QKV


def tile_attention_pa_t_kernel(
    tc, x, freqs_cis, wqkv_words, wqkv_scales, q_norm_w, k_norm_w, out_0, out_1, out_2
):
    nc = tc.nc
    with ExitStack() as ctx:
        const = ctx.enter_context(tc.tile_pool(name="const", bufs=1))
        x_pool = ctx.enter_context(tc.tile_pool(name="x_pool", bufs=LOOKAHEAD + 2))
        work = ctx.enter_context(tc.tile_pool(name="work", bufs=3))
        late = ctx.enter_context(tc.tile_pool(name="late", bufs=NORM_LAG))
        psum_xt = ctx.enter_context(tc.psum_pool(name="psum_xt", bufs=4))
        psum_qkv = ctx.enter_context(tc.psum_pool(name="psum_qkv", bufs=2))
        psum_sum = ctx.enter_context(tc.psum_pool(name="psum_sum", bufs=2))
        ctx.enter_context(tc.manual_schedule())

        x_rows = x.rearrange("b (p t) d -> b p t d", t=POS)
        q_rows = out_0.rearrange("b (p t) h c -> b p t (h c)", t=POS)
        k_rows = out_1.rearrange("b (p t) h c -> b p t (h c)", t=POS)
        v_rows = out_2.rearrange("b (p t) h c -> b p t (h c)", t=POS)

        live = {}

        def load_x(g, pieces=1):
            b, first = divmod(g * GROUP, POS)
            x_tile = x_pool.tile([P, GROUP, DIM], BF16, name="x_tile")
            live["x", g] = x_tile
            count = GROUP // pieces
            for i in range(0, GROUP, count):
                nc.sync.dma_start(
                    out=x_tile[:, i : i + count, :], in_=x_rows[b, :, first + i : first + i + count, :]
                )

        gain_rows = const.tile([P, 2 * HEAD], BF16)
        nc.gpsimd.memset(gain_rows[:], 0.0)
        nc.sync.dma_start(out=gain_rows[0:1, 0:HEAD], in_=q_norm_w.rearrange("(o c) -> o c", o=1))
        nc.sync.dma_start(out=gain_rows[0:1, HEAD : 2 * HEAD], in_=k_norm_w.rearrange("(o c) -> o c", o=1))
        w_scales = const.tile([P, 2, QKV], U8, align_bytes=64)
        nc.vector.memset(w_scales[:].bitcast(I32), 0)
        w_passes = const.tile([P, 2 * (2 * QKV + 1)], U8, align_bytes=64)
        nc.vector.memset(w_passes[:], 0)
        ones = const.tile([P, P], BF16)
        nc.vector.memset(ones[:], 1.0)
        eps = const.tile([P, 1], F32)
        nc.vector.memset(eps[:], EPS)
        ident = const.tile([P, P], F32)
        make_identity(nc, ident[:])
        gather = const.tile([P, P // 2], F32)
        nc.gpsimd.memset(gather[:, VECTORS:], 0.0)
        nc.vector.tensor_reduce(
            out=gather[:, 0:VECTORS],
            in_=ident[:, 0 : CLASSES * VECTORS].rearrange("p (r v) -> p v r", r=CLASSES),
            axis=AXIS.X,
            op=ALU.add,
        )
        w_words = const.tile([P, 2 * QKV], U8)
        nc.sync.dma_start(out=w_words[:].bitcast(I32), in_=wqkv_words[0].bitcast(I32))
        w_bytes = const.tile([P, 2, QKV], U8)
        nc.vector.tensor_copy(out=w_bytes[:], in_=w_words[:].rearrange("p (n b) -> p b n", b=2))
        fc_rows = freqs_cis.rearrange("(p t) j e -> p t j e", t=POS)
        fc_first = const.tile([P, PART, PAIRS, 2], BF16)
        nc.sync.dma_start(out=fc_first[:], in_=fc_rows[:, 0:PART])
        load_x(0, pieces=2)
        fc_rest = const.tile([P, POS - PART, PAIRS, 2], BF16)
        nc.sync.dma_start(out=fc_rest[:], in_=fc_rows[:, PART:POS])
        load_x(1)
        scale_rows = wqkv_scales[0].rearrange("(u q j) n -> q u j n", u=2, j=2)
        for r in range(4):
            nc.sync.dma_start(
                out=w_scales[r:P:32, :, :].bitcast(I32), in_=scale_rows[:, :, r // 2, :].bitcast(I32)
            )
        load_x(2)
        w_halves = const.tile([P, 2, QKV], U8)
        for u in range(2):
            for b in range(2):
                nc.sync.dma_start(
                    out=w_halves[b:P:2, u, :].bitcast(I32),
                    in_=w_bytes[64 * u : 64 * u + 64, b, :].bitcast(I32),
                )
        for g in range(3, LOOKAHEAD):
            load_x(g)

        warm = const.tile([P, 1], F32)
        nc.scalar.activation(
            out=warm[:], in_=eps[:], func=ACT.Abs_reciprocal_sqrt, bias=eps[:, 0:1], scale=1.0
        )
        chunk_squares = []
        for i in range(2):
            sq = const.tile([P, (FOLDS - 1) * CLASSES * VECTORS + P], F32, name="chunk_squares%d" % i)
            nc.gpsimd.memset(sq[:, VECTORS * HEAD :], 0.0)
            chunk_squares.append(sq)

        spread = psum_qkv.tile([P, 2 * HEAD], F32, name="qkv")
        nc.tensor.matmul(out=spread[:], lhsT=ones[:], rhs=gain_rows[:], start=True, stop=True)
        gain_raw = const.tile([P, NORMED, HEAD], BF16)
        nc.vector.tensor_copy(
            out=gain_raw[:, 0:2, :], in_=spread[:, 0:HEAD].unsqueeze(1).to_broadcast([P, 2, HEAD])
        )
        nc.vector.tensor_copy(out=gain_raw[:, 2, :], in_=spread[:, HEAD : 2 * HEAD])
        gain_pairs = gain_raw[:].rearrange("p h (j e) -> p h j e", e=2)
        gain_minus = const.tile([P, NORMED, PAIRS], BF16)
        nc.vector.tensor_scalar_mul(out=gain_minus[:], in0=gain_pairs[:, :, :, 1], scalar1=-1.0)
        tables = {}

        def build_tables(part, engine):
            table_a = const.tile([P, 2, PART, ROT_PAIRS], F32, name="table_a%d" % part)
            table_b = const.tile([P, 2, PART, ROT_PAIRS], F32, name="table_b%d" % part)
            tables[part] = (table_a, table_b)
            shape = [P, PART, NORMED - 1, PAIRS]
            fc = fc_first[:] if part == 0 else fc_rest[:, (part - 1) * PART : part * PART]
            fr = fc[:, :, :, 0].unsqueeze(2).to_broadcast(shape)
            fi = fc[:, :, :, 1].unsqueeze(2).to_broadcast(shape)
            g_even = gain_pairs[:, 1:NORMED, :, 0].unsqueeze(1).to_broadcast(shape)
            g_odd = gain_pairs[:, 1:NORMED, :, 1].unsqueeze(1).to_broadcast(shape)
            g_minus = gain_minus[:, 1:NORMED, :].unsqueeze(1).to_broadcast(shape)
            for table, which, f, g in (
                (table_a, 0, fr, g_even),
                (table_a, 1, fi, g_even),
                (table_b, 0, fi, g_minus),
                (table_b, 1, fr, g_odd),
            ):
                engine.tensor_tensor(
                    out=table[:, which, :, PAIRS:ROT_PAIRS].rearrange(
                        "p t (h j) -> p t h j", h=NORMED - 1
                    ),
                    in0=f,
                    in1=g,
                    op=ALU.mult,
                )
            for table in (table_a, table_b):
                engine.tensor_copy(out=table[:, :, :, 0:PAIRS], in_=table[:, :, :, PAIRS : 2 * PAIRS])

        build_tables(0, nc.vector)
        build_tables(1, nc.vector)

        def expand_w():
            nc.vector.tensor_copy(
                out=w_passes[:].rearrange("p (u m) -> p u m", u=2)[:, :, 0 : 2 * QKV : 2], in_=w_halves[:]
            )

        def transpose_x(g):
            words = live["x", g][:].bitcast(F32)
            for half in range(2):
                xt = psum_xt.tile([P, 2, 2, P], F32, name="xt")
                live["xt", g, half] = xt
                for i in range(2):
                    for u in range(2):
                        nc.tensor.transpose(
                            xt[:, i, u, :], words[:, 2 * half + i, u * P : (u + 1) * P], ident[:]
                        )

        def regroup_x(g):
            grouped = work.tile([P, GROUP * P * 4], BF16, name="grouped", align_bytes=64)
            live["grouped", g] = grouped
            as_words = grouped[:].bitcast(F32).rearrange("p (i r u) -> p i r u", i=GROUP, u=2)
            for half in range(2):
                nc.scalar.copy(
                    out=as_words[:, 2 * half : 2 * half + 2, :, :],
                    in_=live["xt", g, half][:].rearrange("p i u r -> p i r u"),
                )

        def quantise_x(g):
            codes = work.tile([P, GROUP * P], U32, name="codes", align_bytes=64)
            planes = work.tile([P, GROUP * P], U8, name="planes", align_bytes=64)
            live["codes", g] = (codes, planes)
            nc.vector.quantize_mx(
                out=codes[:].bitcast(FP8X4), scales=planes[:], in_=live["grouped", g][:]
            )

        def project(g):
            codes, planes = live["codes", g]
            qkv = psum_qkv.tile([P, GROUP, QKV], F32, name="qkv")
            live["qkv", g] = qkv
            for i in range(GROUP):
                tokens = slice(i * P, (i + 1) * P)
                for u in range(2):
                    nc.tensor.matmul_mx(
                        out=qkv[:, i, :],
                        lhsT=codes[:, tokens].bitcast(FP8X4),
                        lhsT_scale=planes[:, tokens],
                        rhs=w_passes[:, 2 * QKV * u : 2 * QKV * (u + 1)].bitcast(FP4X4),
                        rhs_scale=w_scales[:, u, :],
                        start=u == 0,
                        stop=u == 1,
                    )

        def chunk_tile(name, g, shape):
            c, first = divmod(g * GROUP, CHUNK)
            if (name, c) not in live:
                live[name, c] = work.tile(shape, F32, name=name)
            return live[name, c], slice(first, first + GROUP)

        def square(g):
            qkv = live["qkv", g]
            if g < SUMMED:
                m, half = divmod(g, 2)
                size = GROUP * NORMED
                by_vector = chunk_squares[m % 2][:, 0 : VECTORS * HEAD].rearrange("p (c v) -> p c v", v=VECTORS)
                nc.scalar.activation(
                    out=by_vector[:, :, half * size : (half + 1) * size].rearrange(
                        "p c (h i) -> p h c i", i=GROUP
                    ),
                    in_=qkv[:, :, 0:ROT].rearrange("p i (h c) -> p h c i", c=HEAD),
                    func=ACT.Square,
                    scale=1.0 / math.sqrt(HEAD),
                )
                return
            squares = work.tile([P, GROUP, NORMED, HEAD], F32, name="squares")
            mean_sq = work.tile([P, NORMED, GROUP], F32, name="mean_sq")
            live["squares", g] = squares
            live["mean_sq", g] = mean_sq
            nc.scalar.activation(
                out=squares[:, :, 0:2, :],
                in_=qkv[:, :, 0 : 2 * HEAD].rearrange("p i (h c) -> p i h c", c=HEAD),
                func=ACT.Square,
                scale=1.0 / math.sqrt(HEAD),
            )
            for i in range(GROUP):
                nc.scalar.activation(
                    out=squares[:, i, 2, :],
                    in_=qkv[:, i, 2 * HEAD : ROT],
                    func=ACT.Square,
                    scale=1.0 / math.sqrt(HEAD),
                    accum_out=mean_sq[:, 2, i : i + 1],
                )

        def sum_q(g):
            if g < SUMMED:
                return
            nc.vector.tensor_reduce(
                out=live["mean_sq", g][:, 0:2, :],
                in_=live["squares", g][:, :, 0:2, :].rearrange("p i h c -> p h i c"),
                axis=AXIS.X,
                op=ALU.add,
            )

        def fold(m, first, last):
            if first == 0:
                live["fold", m] = psum_sum.tile([P, P], F32, name="sums")
            for c in range(first, last):
                nc.tensor.matmul(
                    out=live["fold", m][:],
                    lhsT=chunk_squares[m % 2][:, CLASSES * VECTORS * c : CLASSES * VECTORS * c + P],
                    rhs=ident[:],
                    is_transpose=True,
                    start=c == 0,
                    stop=c == FOLDS - 1,
                )

        def copy_fold(m):
            folded = work.tile([P, P], F32, name="folded")
            live["folded", m] = folded
            nc.scalar.copy(out=folded[:], in_=live["fold", m][:])

        def gather_sums(m):
            sums = psum_sum.tile([P, P // 2], F32, name="sums")
            live["sums", m] = sums
            nc.tensor.matmul(out=sums[:], lhsT=live["folded", m][:], rhs=gather[:], start=True, stop=True)

        def invert(g):
            inv_rms = work.tile([P, NORMED, GROUP], F32, name="inv_rms")
            live["inv_rms", g] = inv_rms[:].rearrange("p h i -> p i h")
            if g < SUMMED:
                m, half = divmod(g, 2)
                mean_sq = live["sums", m][:, half * GROUP * NORMED : (half + 1) * GROUP * NORMED]
            else:
                mean_sq = live["mean_sq", g][:].rearrange("p h i -> p (h i)")
            nc.scalar.activation(
                out=inv_rms[:].rearrange("p h i -> p (h i)"),
                in_=mean_sq,
                func=ACT.Abs_reciprocal_sqrt,
                bias=eps[:, 0:1],
                scale=1.0,
            )

        def store_if_full(hbm, staged, g):
            if g >= GROUPS - 2:
                b, first = divmod(g * GROUP, POS)
                rows = slice(g % 2 * GROUP, (g % 2 + 1) * GROUP)
                nc.sync.dma_start(out=hbm[b, :, first : first + GROUP, :], in_=staged[:, rows, :])
            elif g % 2 == 1:
                b, first = divmod((g - 1) * GROUP, POS)
                nc.sync.dma_start(out=hbm[b, :, first : first + CHUNK, :], in_=staged[:])

        def products(g):
            part, first = divmod(g * GROUP % POS, PART)
            table_a, table_b = tables[part]
            pairs = live["qkv", g][:, :, 0:ROT].rearrange("p i (n e) -> p i n e", e=2)
            prod = work.tile([P, 4, GROUP, ROT_PAIRS], F32, name="prod")
            live["prod", g] = prod
            shape = [P, 2, GROUP, ROT_PAIRS]
            nc.vector.tensor_tensor(
                out=prod[:, 0:4:2],
                in0=pairs[:, :, :, 0].unsqueeze(1).to_broadcast(shape),
                in1=table_a[:, :, first : first + GROUP, :],
                op=ALU.mult,
            )
            nc.vector.tensor_tensor(
                out=prod[:, 1:4:2],
                in0=pairs[:, :, :, 1].unsqueeze(1).to_broadcast(shape),
                in1=table_b[:, :, first : first + GROUP, :],
                op=ALU.mult,
            )

        def copy_v(g):
            v_stage, rows = chunk_tile("v_stage", g, [P, CHUNK, HEAD])
            if g % 2 == 1 and 8 < g < SUMMED:
                nc.vector.tensor_copy(out=v_stage[:, rows, :], in_=live["qkv", g][:, :, ROT:QKV])
            else:
                nc.scalar.copy(out=v_stage[:, rows, :], in_=live["qkv", g][:, :, ROT:QKV])
            store_if_full(v_rows, v_stage, g)

        def rotate(g):
            prod = live["prod", g]
            rotated = late.tile([P, GROUP, ROT], F32, name="rotated")
            live["rotated", g] = rotated
            nc.vector.tensor_tensor(
                out=rotated[:].rearrange("p i (n e) -> p (i n) e", e=2),
                in0=prod[:, 0:4:3].rearrange("p e i n -> p (i n) e"),
                in1=prod[:, 1:3].rearrange("p e i n -> p (i n) e"),
                op=ALU.add,
            )

        def norm_q(g):
            q_stage, rows = chunk_tile("q_stage", g, [P, CHUNK, 2 * HEAD])
            engine = nc.vector if g >= VECTOR_NORMS else nc.gpsimd
            count = Q_GPSIMD if g < VECTOR_NORMS and g % 2 == 0 else GROUP
            engine.tensor_tensor(
                out=q_stage[:, rows.start : rows.start + count, :].rearrange("p i (h c) -> p i h c", c=HEAD),
                in0=live["rotated", g][:, 0:count, 0 : 2 * HEAD].rearrange("p i (h c) -> p i h c", c=HEAD),
                in1=live["inv_rms", g][:, 0:count, 0:2].unsqueeze(3).to_broadcast([P, count, 2, HEAD]),
                op=ALU.mult,
            )

        def norm_q_scalar(g):
            q_stage, rows = chunk_tile("q_stage", g, [P, CHUNK, 2 * HEAD])
            if g < VECTOR_NORMS and g % 2 == 0:
                for i in range(Q_GPSIMD, GROUP):
                    for h in range(2):
                        nc.scalar.activation(
                            out=q_stage[:, rows.start + i, h * HEAD : (h + 1) * HEAD],
                            in_=live["rotated", g][:, i, h * HEAD : (h + 1) * HEAD],
                            func=ACT.Copy,
                            scale=live["inv_rms", g][:, i, h : h + 1],
                        )
            store_if_full(q_rows, q_stage, g)

        def norm_k_scalar(g):
            k_stage, rows = chunk_tile("k_stage", g, [P, CHUNK, HEAD])
            for i in range(K_SCALAR):
                nc.scalar.activation(
                    out=k_stage[:, rows.start + i, :],
                    in_=live["rotated", g][:, i, 2 * HEAD : ROT],
                    func=ACT.Copy,
                    scale=live["inv_rms", g][:, i, 2:3],
                )

        def store_k(g):
            k_stage, rows = chunk_tile("k_stage", g, [P, CHUNK, HEAD])
            store_if_full(k_rows, k_stage, g)

        def run(stage_fn, g):
            if 0 <= g < GROUPS:
                stage_fn(g)

        def run_chunk(stage_fn, g, *rest):
            if 0 <= g < SUMMED and g % 2 == 1:
                stage_fn(g // 2, *rest)

        def norm_group(step):
            return [g for g in range(GROUPS) if min(g + (NORM_LAG if g < SUMMED else 3), GROUPS + 2) == step]

        transpose_x(0)
        for step in range(GROUPS + 3):
            run(load_x, step + LOOKAHEAD)
            run(transpose_x, step + 1)
            run_chunk(fold, step - FOLD_LAG, 0, FOLDS)
            run(quantise_x, step - 1)
            if step == 1:
                expand_w()
            if 2 <= step + 1 < TABLE_PARTS:
                build_tables(step + 1, nc.vector)
            run(project, step - 1)
            run_chunk(gather_sums, step - FOLD_LAG - 1)
            run(rotate, step - 3)
            run(square, step - 2)
            run(copy_v, step - 2)
            for g in norm_group(step):
                invert(g)
            for g in norm_group(step):
                if g < VECTOR_NORMS:
                    norm_q(g)
            run(regroup_x, step)
            run_chunk(copy_fold, step - FOLD_LAG)
            for g in norm_group(step):
                norm_k_scalar(g)
                store_k(g)
            run(products, step - 2)
            run(sum_q, step - 2)
            for g in norm_group(step):
                if g >= VECTOR_NORMS:
                    norm_q(g)
                norm_q_scalar(g)
